import numpy as np
import ml_dtypes


def mxq(x, axis, fmt="e4m3"):
    dtype, down = {"e4m3": (ml_dtypes.float8_e4m3fn, 7), "e5m2": (ml_dtypes.float8_e5m2, 14)}[fmt]
    v = np.moveaxis(np.asarray(x, np.float32).astype(ml_dtypes.bfloat16).astype(np.float64), axis, -1)
    blocks = v.reshape(v.shape[:-1] + (-1, 32))
    amax = np.abs(blocks).max(-1, keepdims=True)
    byte = np.maximum(np.where(amax > 0, np.frexp(amax)[1] - 1 + 127, 0) - down, 1)
    scale = np.exp2(byte - 127.0)
    codes = (blocks / scale).astype(np.float32).astype(dtype).astype(np.float64)
    return np.moveaxis((codes * scale).reshape(v.shape), -1, axis)


WIDE = False


def mx_kscale(k):
    if not WIDE:
        return np.ones(k)
    levels = np.array([10, -10, 5, -5, 0])
    a = np.random.permutation(np.resize(levels, k // 512 * 4)).reshape(k // 512, 4)
    idx = np.arange(k)
    return np.exp2(a[idx // 512, idx % 128 // 32])


BF16 = ml_dtypes.bfloat16


def bf(x):
    return np.asarray(x, np.float32).astype(BF16)


def f64(x):
    return np.asarray(x).astype(np.float64)


B, CI, CO, OH, OW, K = 128, 128, 128, 6, 6, 4
STRIDE = 1
IH, IW = (OH - 1) * STRIDE + K, (OW - 1) * STRIDE + K
P = OH * OW
KC = CI * K * K


def extract_patches(x, out_h, out_w, k, stride):
    rows = []
    for di in range(k):
        cols = []
        for dj in range(k):
            cols.append(x[:, :, di:di + out_h * stride:stride, dj:dj + out_w * stride:stride])
        rows.append(np.stack(cols, axis=2))
    return np.stack(rows, axis=2)


def setup_inputs():
    s = mx_kscale(KC).reshape(CI, K * K)[:, 0]
    return {"in_spikes": bf(np.random.uniform(0.0, 1.0, (B, CI, IH, IW)) * s[None, :, None, None]),
            "weights": bf(np.random.standard_normal((OH, OW, CI, K, K, CO)) * 1.5 / np.sqrt(KC) / s[None, None, :, None, None, None])}


def reference(in_spikes, weights):
    out_h, out_w, _, k, _, _ = weights.shape
    patches = extract_patches(f64(in_spikes), out_h, out_w, k, STRIDE)
    p = patches.reshape(B, KC, P).transpose(2, 0, 1)
    w = f64(weights).reshape(P, KC, CO)
    out = mxq(p, 2, "e4m3") @ mxq(w, 1, "e4m3")
    return out.transpose(1, 2, 0).reshape(B, CO, OH, OW)

@@ -1,0 +1,148 @@
+from contextlib import ExitStack
+
+from concourse import mybir
+from concourse.masks import make_identity
+
+BF16 = mybir.dt.bfloat16
+F32 = mybir.dt.float32
+U32 = mybir.dt.uint32
+U8 = mybir.dt.uint8
+FP8X4 = mybir.dt.float8_e4m3fn_x4
+
+P = 128
+IMG = 9
+OUT = 6
+WIN = 4
+PASSES = 4
+PAIR = 2
+CHUNKS = PAIR * PASSES
+PAIRS_IN_ROW = OUT // PAIR
+ROW_COLS = 8
+ROW_WORDS = ROW_COLS // 2
+K_SCALAR = 48
+
+FLOPS = 2 * P * (P * WIN * WIN) * P * OUT * OUT
+
+
+def tile_stdpconvinhibit_kernel(tc, in_spikes, weights, out):
+    nc = tc.nc
+    w_view = weights.rearrange("i j (g c) u v k -> (c u) (i j g) (v k)", g=PASSES)
+
+    with ExitStack() as stack:
+        keep = stack.enter_context(tc.tile_pool(name="keep", bufs=1))
+        rows_pool = stack.enter_context(tc.tile_pool(name="rows", bufs=2))
+        w_raw_pool = stack.enter_context(tc.tile_pool(name="w_raw", bufs=4))
+        w_grouped_pool = stack.enter_context(tc.tile_pool(name="w_grouped", bufs=3))
+        w_mx_pool = stack.enter_context(tc.tile_pool(name="w_mx", bufs=3))
+        patch_pool = stack.enter_context(tc.tile_pool(name="patch", bufs=3))
+        patch_mx_pool = stack.enter_context(tc.tile_pool(name="patch_mx", bufs=3))
+        planes_pool = stack.enter_context(tc.psum_pool(name="planes", bufs=6))
+        acc_pool = stack.enter_context(tc.psum_pool(name="acc", bufs=2))
+
+        def load_weights(pair):
+            w_raw = w_raw_pool.tile([P, CHUNKS, WIN, P], BF16, name="w_raw")
+            nc.sync.dma_start(
+                out=w_raw[:].rearrange("p n v k -> p n (v k)"),
+                in_=w_view[:, pair * CHUNKS : (pair + 1) * CHUNKS, :],
+            )
+            return w_raw
+
+        first_w_raw = load_weights(0)
+        image = keep.tile([P, P, IMG, IMG], BF16, name="image")
+        nc.sync.dma_start(
+            out=image[:].rearrange("b c h w -> b (c h w)"),
+            in_=in_spikes.rearrange("b c h w -> b (c h w)"),
+        )
+        identity = keep.tile([P, P], F32, name="identity")
+        make_identity(nc, identity[:])
+        result = keep.tile([P, P, OUT * OUT], F32, name="result")
+
+        acc = None
+        for i in range(OUT):
+            rows = rows_pool.tile([P, 2, P * WIN, ROW_COLS], BF16, name="rows")
+            for first in range(2):
+                nc.vector.tensor_copy(
+                    out=rows[:, first].rearrange("b (c u) w -> b c u w", u=WIN),
+                    in_=image[:, :, i : i + WIN, first : first + ROW_COLS],
+                )
+            row_words = (
+                rows[:]
+                .rearrange("b f m w -> b (f m w)")
+                .bitcast(F32)
+                .rearrange("b (f m a) -> b f m a", f=2, a=ROW_WORDS)
+            )
+
+            for s in range(PAIRS_IN_ROW):
+                pair = i * PAIRS_IN_ROW + s
+
+                w_raw = first_w_raw if pair == 0 else load_weights(pair)
+                w_grouped = w_grouped_pool.tile([P, CHUNKS, P, WIN], BF16, name="w_grouped", align_bytes=64)
+                nc.scalar.copy(
+                    out=w_grouped[:, :, 0:K_SCALAR, :],
+                    in_=w_raw[:, :, :, 0:K_SCALAR].rearrange("p n v k -> p n k v"),
+                )
+                nc.vector.tensor_copy(
+                    out=w_grouped[:, :, K_SCALAR:P, :].rearrange("p n (q r) v -> p n q v r", r=4),
+                    in_=w_raw[:, :, :, K_SCALAR:P].rearrange("p n v (q r) -> p n q v r", r=4),
+                )
+                w_codes = w_mx_pool.tile([P, CHUNKS * P], U32, name="w_codes", align_bytes=64)
+                w_scales = w_mx_pool.tile([P, CHUNKS * P], U8, name="w_scales", align_bytes=64)
+                nc.vector.quantize_mx(
+                    out=w_codes[:].bitcast(FP8X4),
+                    scales=w_scales[:],
+                    in_=w_grouped[:].rearrange("p n k v -> p (n k v)"),
+                )
+
+                patches = patch_pool.tile([P, PAIR, PASSES, P, WIN], BF16, name="patches", align_bytes=64)
+                patch_words = (
+                    patches[:]
+                    .rearrange("p t g b v -> p (t g b v)")
+                    .bitcast(F32)
+                    .rearrange("p (t g b h) -> p t g b h", t=PAIR, g=PASSES, h=2)
+                )
+                for g in range(PASSES):
+                    planes = planes_pool.tile([P, PAIR, 2, P], F32, name="planes")
+                    for t in range(PAIR):
+                        for h in range(2):
+                            nc.tensor.transpose(
+                                planes[:, t, h, :],
+                                row_words[:, t, g * P : (g + 1) * P, s + h],
+                                identity[:],
+                            )
+                    nc.scalar.copy(
+                        out=patch_words[:, :, g, :, :],
+                        in_=planes[:].rearrange("p t h b -> p t b h"),
+                    )
+                patch_codes = patch_mx_pool.tile([P, CHUNKS * P], U32, name="patch_codes", align_bytes=64)
+                patch_scales = patch_mx_pool.tile([P, CHUNKS * P], U8, name="patch_scales", align_bytes=64)
+                nc.vector.quantize_mx(
+                    out=patch_codes[:].bitcast(FP8X4),
+                    scales=patch_scales[:],
+                    in_=patches[:].rearrange("p t g b v -> p (t g b v)"),
+                )
+
+                if pair % 2 == 0:
+                    acc = acc_pool.tile([P, 2 * PAIR, P], F32, name="acc")
+                for t in range(PAIR):
+                    for g in range(PASSES):
+                        cols = slice((t * PASSES + g) * P, (t * PASSES + g + 1) * P)
+                        nc.tensor.matmul_mx(
+                            out=acc[:, (pair % 2) * PAIR + t, :],
+                            lhsT=patch_codes[:, cols].bitcast(FP8X4),
+                            lhsT_scale=patch_scales[:, cols],
+                            rhs=w_codes[:, cols].bitcast(FP8X4),
+                            rhs_scale=w_scales[:, cols],
+                            start=(g == 0),
+                            stop=(g == PASSES - 1),
+                        )
+                if pair % 2 == 1:
+                    first_pos = (pair - 1) * PAIR
+                    nc.scalar.copy(
+                        out=result[:, :, first_pos : first_pos + 2 * PAIR],
+                        in_=acc[:].rearrange("b q k -> b k q"),
+                    )
+
+        nc.sync.dma_start(
+            out=out.rearrange("b k i j -> b (k i j)"),
+            in_=result[:].rearrange("b k q -> b (k q)"),
+        )

@@ -17,6 +17,7 @@ PASSES = 4
 PAIR = 2
 CHUNKS = PAIR * PASSES
 PAIRS_IN_ROW = OUT // PAIR
+PAIRS = OUT * PAIRS_IN_ROW
 ROW_COLS = 8
 ROW_WORDS = ROW_COLS // 2
 K_SCALAR = 48
@@ -26,121 +27,171 @@ FLOPS = 2 * P * (P * WIN * WIN) * P * OUT * OUT
 
 def tile_stdpconvinhibit_kernel(tc, in_spikes, weights, out):
     nc = tc.nc
-    w_view = weights.rearrange("i j (g c) u v k -> (c u) (i j g) (v k)", g=PASSES)
+    w_view = weights.rearrange("i j (g c) u v k -> u c (i j g) (v k)", g=PASSES)
+    channels = P // PASSES
 
     with ExitStack() as stack:
         keep = stack.enter_context(tc.tile_pool(name="keep", bufs=1))
-        rows_pool = stack.enter_context(tc.tile_pool(name="rows", bufs=2))
         w_raw_pool = stack.enter_context(tc.tile_pool(name="w_raw", bufs=4))
-        w_grouped_pool = stack.enter_context(tc.tile_pool(name="w_grouped", bufs=3))
+        w_grouped_pool = stack.enter_context(tc.tile_pool(name="w_grouped", bufs=2))
         w_mx_pool = stack.enter_context(tc.tile_pool(name="w_mx", bufs=3))
-        patch_pool = stack.enter_context(tc.tile_pool(name="patch", bufs=3))
-        patch_mx_pool = stack.enter_context(tc.tile_pool(name="patch_mx", bufs=3))
+        patch_pool = stack.enter_context(tc.tile_pool(name="patch", bufs=2))
+        patch_mx_pool = stack.enter_context(tc.tile_pool(name="patch_mx", bufs=4))
         planes_pool = stack.enter_context(tc.psum_pool(name="planes", bufs=6))
         acc_pool = stack.enter_context(tc.psum_pool(name="acc", bufs=2))
+        stack.enter_context(tc.manual_schedule())
+
+        image = keep.tile([P, P, IMG, IMG], BF16, name="image")
+        identity = keep.tile([P, P], F32, name="identity")
+        result = keep.tile([P, P, OUT * OUT], F32, name="result")
+        ring = keep.tile([P, 2, P * WIN, ROW_COLS], BF16, name="ring")
+        ring_words = (
+            ring[:]
+            .rearrange("b f m w -> b (f m w)")
+            .bitcast(F32)
+            .rearrange("b (f m a) -> b f m a", f=2, a=ROW_WORDS)
+        )
+        w_raw, w_grouped, w_codes, w_scales = {}, {}, {}, {}
+        planes, patches, patch_codes, patch_scales, acc = {}, {}, {}, {}, {}
+
+        def load_image():
+            for g in range(PASSES):
+                some = slice(g * channels, (g + 1) * channels)
+                nc.sync.dma_start(
+                    out=image[:, some].rearrange("b c h w -> b (c h w)"),
+                    in_=in_spikes[:, some].rearrange("b c h w -> b (c h w)"),
+                )
 
         def load_weights(pair):
-            w_raw = w_raw_pool.tile([P, CHUNKS, WIN, P], BF16, name="w_raw")
-            nc.sync.dma_start(
-                out=w_raw[:].rearrange("p n v k -> p n (v k)"),
-                in_=w_view[:, pair * CHUNKS : (pair + 1) * CHUNKS, :],
+            i = pair // PAIRS_IN_ROW
+            w_raw[pair] = w_raw_pool.tile([P, CHUNKS, WIN, P], BF16, name="w_raw")
+            for u in range(WIN):
+                r = (i + u) % WIN
+                nc.sync.dma_start(
+                    out=w_raw[pair][r:P:WIN].rearrange("p n v k -> p n (v k)"),
+                    in_=w_view[u, :, pair * CHUNKS : (pair + 1) * CHUNKS, :],
+                )
+
+        def regroup_weights(pair):
+            w_grouped[pair] = w_grouped_pool.tile([P, CHUNKS, P, WIN], BF16, name="w_grouped", align_bytes=64)
+            nc.scalar.copy(
+                out=w_grouped[pair][:, :, 0:K_SCALAR, :],
+                in_=w_raw[pair][:, :, :, 0:K_SCALAR].rearrange("p n v k -> p n k v"),
             )
-            return w_raw
+            nc.vector.tensor_copy(
+                out=w_grouped[pair][:, :, K_SCALAR:P, :].rearrange("p n (q r) v -> p n q v r", r=4),
+                in_=w_raw[pair][:, :, :, K_SCALAR:P].rearrange("p n v (q r) -> p n q v r", r=4),
+            )
 
-        first_w_raw = load_weights(0)
-        image = keep.tile([P, P, IMG, IMG], BF16, name="image")
-        nc.sync.dma_start(
-            out=image[:].rearrange("b c h w -> b (c h w)"),
-            in_=in_spikes.rearrange("b c h w -> b (c h w)"),
-        )
-        identity = keep.tile([P, P], F32, name="identity")
-        make_identity(nc, identity[:])
-        result = keep.tile([P, P, OUT * OUT], F32, name="result")
+        def quantise_weights(pair):
+            w_codes[pair] = w_mx_pool.tile([P, CHUNKS * P], U32, name="w_codes", align_bytes=64)
+            w_scales[pair] = w_mx_pool.tile([P, CHUNKS * P], U8, name="w_scales", align_bytes=64)
+            nc.vector.quantize_mx(
+                out=w_codes[pair][:].bitcast(FP8X4),
+                scales=w_scales[pair][:],
+                in_=w_grouped[pair][:].rearrange("p n k v -> p (n k v)"),
+            )
 
-        acc = None
-        for i in range(OUT):
-            rows = rows_pool.tile([P, 2, P * WIN, ROW_COLS], BF16, name="rows")
+        def fill_ring():
+            for g in range(PASSES):
+                for first in range(2):
+                    nc.vector.tensor_copy(
+                        out=ring[:, first, g * P : (g + 1) * P, :].rearrange("b (c r) w -> b c r w", r=WIN),
+                        in_=image[:, g * channels : (g + 1) * channels, 0:WIN, first : first + ROW_COLS],
+                    )
+
+        def turn_ring(i):
+            new_row = i + WIN - 1
             for first in range(2):
                 nc.vector.tensor_copy(
-                    out=rows[:, first].rearrange("b (c u) w -> b c u w", u=WIN),
-                    in_=image[:, :, i : i + WIN, first : first + ROW_COLS],
+                    out=ring[:, first].rearrange("b (c r) w -> b c r w", r=WIN)[:, :, new_row % WIN, :],
+                    in_=image[:, :, new_row, first : first + ROW_COLS],
                 )
-            row_words = (
-                rows[:]
-                .rearrange("b f m w -> b (f m w)")
+
+        def transpose_words(pair):
+            s = pair % PAIRS_IN_ROW
+            for g in range(PASSES):
+                planes[pair, g] = planes_pool.tile([P, PAIR, 2, P], F32, name="planes")
+                for t in range(PAIR):
+                    for h in range(2):
+                        nc.tensor.transpose(
+                            planes[pair, g][:, t, h, :],
+                            ring_words[:, t, g * P : (g + 1) * P, s + h],
+                            identity[:],
+                        )
+
+        def copy_out_patches(pair):
+            patches[pair] = patch_pool.tile([P, PAIR, PASSES, P, WIN], BF16, name="patches", align_bytes=64)
+            patch_words = (
+                patches[pair][:]
+                .rearrange("p t g b v -> p (t g b v)")
                 .bitcast(F32)
-                .rearrange("b (f m a) -> b f m a", f=2, a=ROW_WORDS)
+                .rearrange("p (t g b h) -> p t g b h", t=PAIR, g=PASSES, h=2)
+            )
+            for g in range(PASSES):
+                nc.scalar.copy(
+                    out=patch_words[:, :, g, :, :],
+                    in_=planes[pair, g][:].rearrange("p t h b -> p t b h"),
+                )
+
+        def quantise_patches(pair):
+            patch_codes[pair] = patch_mx_pool.tile([P, CHUNKS * P], U32, name="patch_codes", align_bytes=64)
+            patch_scales[pair] = patch_mx_pool.tile([P, CHUNKS * P], U8, name="patch_scales", align_bytes=64)
+            nc.vector.quantize_mx(
+                out=patch_codes[pair][:].bitcast(FP8X4),
+                scales=patch_scales[pair][:],
+                in_=patches[pair][:].rearrange("p t g b v -> p (t g b v)"),
             )
 
-            for s in range(PAIRS_IN_ROW):
-                pair = i * PAIRS_IN_ROW + s
-
-                w_raw = first_w_raw if pair == 0 else load_weights(pair)
-                w_grouped = w_grouped_pool.tile([P, CHUNKS, P, WIN], BF16, name="w_grouped", align_bytes=64)
-                nc.scalar.copy(
-                    out=w_grouped[:, :, 0:K_SCALAR, :],
-                    in_=w_raw[:, :, :, 0:K_SCALAR].rearrange("p n v k -> p n k v"),
-                )
-                nc.vector.tensor_copy(
-                    out=w_grouped[:, :, K_SCALAR:P, :].rearrange("p n (q r) v -> p n q v r", r=4),
-                    in_=w_raw[:, :, :, K_SCALAR:P].rearrange("p n v (q r) -> p n q v r", r=4),
-                )
-                w_codes = w_mx_pool.tile([P, CHUNKS * P], U32, name="w_codes", align_bytes=64)
-                w_scales = w_mx_pool.tile([P, CHUNKS * P], U8, name="w_scales", align_bytes=64)
-                nc.vector.quantize_mx(
-                    out=w_codes[:].bitcast(FP8X4),
-                    scales=w_scales[:],
-                    in_=w_grouped[:].rearrange("p n k v -> p (n k v)"),
-                )
-
-                patches = patch_pool.tile([P, PAIR, PASSES, P, WIN], BF16, name="patches", align_bytes=64)
-                patch_words = (
-                    patches[:]
-                    .rearrange("p t g b v -> p (t g b v)")
-                    .bitcast(F32)
-                    .rearrange("p (t g b h) -> p t g b h", t=PAIR, g=PASSES, h=2)
-                )
+        def multiply(pair):
+            bank = pair // 2
+            if pair % 2 == 0:
+                acc[bank] = acc_pool.tile([P, 2 * PAIR, P], F32, name="acc")
+            for t in range(PAIR):
                 for g in range(PASSES):
-                    planes = planes_pool.tile([P, PAIR, 2, P], F32, name="planes")
-                    for t in range(PAIR):
-                        for h in range(2):
-                            nc.tensor.transpose(
-                                planes[:, t, h, :],
-                                row_words[:, t, g * P : (g + 1) * P, s + h],
-                                identity[:],
-                            )
-                    nc.scalar.copy(
-                        out=patch_words[:, :, g, :, :],
-                        in_=planes[:].rearrange("p t h b -> p t b h"),
+                    cols = slice((t * PASSES + g) * P, (t * PASSES + g + 1) * P)
+                    nc.tensor.matmul_mx(
+                        out=acc[bank][:, (pair % 2) * PAIR + t, :],
+                        lhsT=patch_codes[pair][:, cols].bitcast(FP8X4),
+                        lhsT_scale=patch_scales[pair][:, cols],
+                        rhs=w_codes[pair][:, cols].bitcast(FP8X4),
+                        rhs_scale=w_scales[pair][:, cols],
+                        start=(g == 0),
+                        stop=(g == PASSES - 1),
                     )
-                patch_codes = patch_mx_pool.tile([P, CHUNKS * P], U32, name="patch_codes", align_bytes=64)
-                patch_scales = patch_mx_pool.tile([P, CHUNKS * P], U8, name="patch_scales", align_bytes=64)
-                nc.vector.quantize_mx(
-                    out=patch_codes[:].bitcast(FP8X4),
-                    scales=patch_scales[:],
-                    in_=patches[:].rearrange("p t g b v -> p (t g b v)"),
-                )
 
-                if pair % 2 == 0:
-                    acc = acc_pool.tile([P, 2 * PAIR, P], F32, name="acc")
-                for t in range(PAIR):
-                    for g in range(PASSES):
-                        cols = slice((t * PASSES + g) * P, (t * PASSES + g + 1) * P)
-                        nc.tensor.matmul_mx(
-                            out=acc[:, (pair % 2) * PAIR + t, :],
-                            lhsT=patch_codes[:, cols].bitcast(FP8X4),
-                            lhsT_scale=patch_scales[:, cols],
-                            rhs=w_codes[:, cols].bitcast(FP8X4),
-                            rhs_scale=w_scales[:, cols],
-                            start=(g == 0),
-                            stop=(g == PASSES - 1),
-                        )
-                if pair % 2 == 1:
-                    first_pos = (pair - 1) * PAIR
-                    nc.scalar.copy(
-                        out=result[:, :, first_pos : first_pos + 2 * PAIR],
-                        in_=acc[:].rearrange("b q k -> b k q"),
-                    )
+        def copy_out_result(bank):
+            nc.scalar.copy(
+                out=result[:, :, bank * 2 * PAIR : (bank + 1) * 2 * PAIR],
+                in_=acc[bank][:].rearrange("b q k -> b k q"),
+            )
+
+        def exists(pair):
+            return 0 <= pair < PAIRS
+
+        make_identity(nc, identity[:])
+        load_image()
+        for step in range(-4, PAIRS + 1):
+            if exists(step + 4):
+                load_weights(step + 4)
+            if exists(step - 1):
+                multiply(step - 1)
+            if exists(step + 1):
+                quantise_patches(step + 1)
+            if exists(step + 3):
+                if step + 3 == 0:
+                    fill_ring()
+                elif (step + 3) % PAIRS_IN_ROW == 0:
+                    turn_ring((step + 3) // PAIRS_IN_ROW)
+                transpose_words(step + 3)
+            if exists(step + 2):
+                copy_out_patches(step + 2)
+            if exists(step):
+                quantise_weights(step)
+            if exists(step + 1):
+                regroup_weights(step + 1)
+            if exists(step - 1) and (step - 1) % 2 == 1:
+                copy_out_result((step - 1) // 2)
 
         nc.sync.dma_start(
             out=out.rearrange("b k i j -> b (k i j)"),

@@ -20,7 +20,7 @@ PAIRS_IN_ROW = OUT // PAIR
 PAIRS = OUT * PAIRS_IN_ROW
 ROW_COLS = 8
 ROW_WORDS = ROW_COLS // 2
-K_SCALAR = 48
+K_SCALAR = 40
 
 FLOPS = 2 * P * (P * WIN * WIN) * P * OUT * OUT
 

@@ -20,7 +20,7 @@ PAIRS_IN_ROW = OUT // PAIR
 PAIRS = OUT * PAIRS_IN_ROW
 ROW_COLS = 8
 ROW_WORDS = ROW_COLS // 2
-K_SCALAR = 40
+K_SCALAR = 48
 
 FLOPS = 2 * P * (P * WIN * WIN) * P * OUT * OUT
 
@@ -75,8 +75,8 @@ def tile_stdpconvinhibit_kernel(tc, in_spikes, weights, out):
         def regroup_weights(pair):
             w_grouped[pair] = w_grouped_pool.tile([P, CHUNKS, P, WIN], BF16, name="w_grouped", align_bytes=64)
             nc.scalar.copy(
-                out=w_grouped[pair][:, :, 0:K_SCALAR, :],
-                in_=w_raw[pair][:, :, :, 0:K_SCALAR].rearrange("p n v k -> p n k v"),
+                out=w_grouped[pair][:, :, 0:K_SCALAR, :].rearrange("p n (q r) v -> p n q v r", r=4),
+                in_=w_raw[pair][:, :, :, 0:K_SCALAR].rearrange("p n v (q r) -> p n q v r", r=4),
             )
             nc.vector.tensor_copy(
                 out=w_grouped[pair][:, :, K_SCALAR:P, :].rearrange("p n (q r) v -> p n q v r", r=4),

@@ -20,7 +20,7 @@ PAIRS_IN_ROW = OUT // PAIR
 PAIRS = OUT * PAIRS_IN_ROW
 ROW_COLS = 8
 ROW_WORDS = ROW_COLS // 2
-K_SCALAR = 48
+K_SCALAR = 76
 
 FLOPS = 2 * P * (P * WIN * WIN) * P * OUT * OUT
 
@@ -33,10 +33,10 @@ def tile_stdpconvinhibit_kernel(tc, in_spikes, weights, out):
     with ExitStack() as stack:
         keep = stack.enter_context(tc.tile_pool(name="keep", bufs=1))
         w_raw_pool = stack.enter_context(tc.tile_pool(name="w_raw", bufs=4))
-        w_grouped_pool = stack.enter_context(tc.tile_pool(name="w_grouped", bufs=2))
+        w_grouped_pool = stack.enter_context(tc.tile_pool(name="w_grouped", bufs=3))
         w_mx_pool = stack.enter_context(tc.tile_pool(name="w_mx", bufs=3))
-        patch_pool = stack.enter_context(tc.tile_pool(name="patch", bufs=2))
-        patch_mx_pool = stack.enter_context(tc.tile_pool(name="patch_mx", bufs=4))
+        x_pool = stack.enter_context(tc.tile_pool(name="x", bufs=2))
+        patch_mx_pool = stack.enter_context(tc.tile_pool(name="patch_mx", bufs=6))
         planes_pool = stack.enter_context(tc.psum_pool(name="planes", bufs=6))
         acc_pool = stack.enter_context(tc.psum_pool(name="acc", bufs=2))
         stack.enter_context(tc.manual_schedule())
@@ -44,15 +44,29 @@ def tile_stdpconvinhibit_kernel(tc, in_spikes, weights, out):
         image = keep.tile([P, P, IMG, IMG], BF16, name="image")
         identity = keep.tile([P, P], F32, name="identity")
         result = keep.tile([P, P, OUT * OUT], F32, name="result")
-        ring = keep.tile([P, 2, P * WIN, ROW_COLS], BF16, name="ring")
-        ring_words = (
-            ring[:]
+        top = keep.tile([P, 2, P * WIN, ROW_COLS], BF16, name="top")
+        top_words = (
+            top[:]
             .rearrange("b f m w -> b (f m w)")
             .bitcast(F32)
             .rearrange("b (f m a) -> b f m a", f=2, a=ROW_WORDS)
         )
+        rows = keep.tile([P, IMG - WIN, 2, P, ROW_COLS], BF16, name="rows")
+        rows_words = (
+            rows[:]
+            .rearrange("b r f c w -> b (r f c w)")
+            .bitcast(F32)
+            .rearrange("b (r f c a) -> b r f c a", r=IMG - WIN, f=2, a=ROW_WORDS)
+        )
+        ring = keep.tile([P, OUT, PASSES, P * WIN], BF16, name="ring", align_bytes=64)
+        ring_words = (
+            ring[:]
+            .rearrange("p j g n -> p (j g n)")
+            .bitcast(F32)
+            .rearrange("p (j g b h) -> p j g b h", j=OUT, g=PASSES, h=2)
+        )
         w_raw, w_grouped, w_codes, w_scales = {}, {}, {}, {}
-        planes, patches, patch_codes, patch_scales, acc = {}, {}, {}, {}, {}
+        planes, x_rows, x_words, patch_codes, patch_scales, acc = {}, {}, {}, {}, {}, {}
 
         def load_image():
             for g in range(PASSES):
@@ -92,55 +106,73 @@ def tile_stdpconvinhibit_kernel(tc, in_spikes, weights, out):
                 in_=w_grouped[pair][:].rearrange("p n k v -> p (n k v)"),
             )
 
-        def fill_ring():
-            for g in range(PASSES):
-                for first in range(2):
-                    nc.vector.tensor_copy(
-                        out=ring[:, first, g * P : (g + 1) * P, :].rearrange("b (c r) w -> b c r w", r=WIN),
-                        in_=image[:, g * channels : (g + 1) * channels, 0:WIN, first : first + ROW_COLS],
-                    )
+        def copy_words(on_vector, dst, src):
+            if on_vector:
+                nc.vector.tensor_copy(out=dst, in_=src)
+            else:
+                nc.scalar.copy(out=dst, in_=src)
 
-        def turn_ring(i):
-            new_row = i + WIN - 1
+        def first_window(g):
+            some = slice(g * channels, (g + 1) * channels)
             for first in range(2):
                 nc.vector.tensor_copy(
-                    out=ring[:, first].rearrange("b (c r) w -> b c r w", r=WIN)[:, :, new_row % WIN, :],
-                    in_=image[:, :, new_row, first : first + ROW_COLS],
+                    out=top[:, first, g * P : (g + 1) * P, :].rearrange("b (c r) w -> b c r w", r=WIN),
+                    in_=image[:, some, 0:WIN, first : first + ROW_COLS],
                 )
-
-        def transpose_words(pair):
-            s = pair % PAIRS_IN_ROW
-            for g in range(PASSES):
-                planes[pair, g] = planes_pool.tile([P, PAIR, 2, P], F32, name="planes")
+            for s in range(PAIRS_IN_ROW):
+                planes[g, s] = planes_pool.tile([P, PAIR, 2, P], F32, name="planes")
                 for t in range(PAIR):
                     for h in range(2):
-                        nc.tensor.transpose(
-                            planes[pair, g][:, t, h, :],
-                            ring_words[:, t, g * P : (g + 1) * P, s + h],
-                            identity[:],
-                        )
+                        nc.tensor.transpose(planes[g, s][:, t, h, :], top_words[:, t, g * P : (g + 1) * P, s + h], identity[:])
+            for s in range(PAIRS_IN_ROW):
+                copy_words(
+                    s == 9,
+                    ring_words[:, PAIR * s : PAIR * (s + 1), g, :, :],
+                    planes[g, s][:].rearrange("p t h b -> p t b h"),
+                )
 
-        def copy_out_patches(pair):
-            patches[pair] = patch_pool.tile([P, PAIR, PASSES, P, WIN], BF16, name="patches", align_bytes=64)
-            patch_words = (
-                patches[pair][:]
-                .rearrange("p t g b v -> p (t g b v)")
-                .bitcast(F32)
-                .rearrange("p (t g b h) -> p t g b h", t=PAIR, g=PASSES, h=2)
+        def align_row(row):
+            for first in range(2):
+                nc.vector.tensor_copy(
+                    out=rows[:, row - WIN, first, :, :],
+                    in_=image[:, :, row, first : first + ROW_COLS],
+                )
+
+        def transpose_row(row, s):
+            planes[row, s] = planes_pool.tile([P, PAIR, 2, P], F32, name="planes")
+            for t in range(PAIR):
+                for h in range(2):
+                    nc.tensor.transpose(planes[row, s][:, t, h, :], rows_words[:, row - WIN, t, :, s + h], identity[:])
+
+        def copy_out_row(row, s):
+            if s == 0:
+                x_rows[row] = x_pool.tile([P, OUT, P, WIN], BF16, name="x_row")
+                x_words[row] = (
+                    x_rows[row][:]
+                    .rearrange("c j b v -> c (j b v)")
+                    .bitcast(F32)
+                    .rearrange("c (j b h) -> c j b h", j=OUT, h=2)
+                )
+            nc.scalar.copy(
+                out=x_words[row][:, PAIR * s : PAIR * (s + 1), :, :],
+                in_=planes[row, s][:].rearrange("c t h b -> c t b h"),
             )
+
+        def spread_row(row):
             for g in range(PASSES):
-                nc.scalar.copy(
-                    out=patch_words[:, :, g, :, :],
-                    in_=planes[pair, g][:].rearrange("p t h b -> p t b h"),
+                nc.sync.dma_start(
+                    out=ring[row % WIN : P : WIN, :, g, :],
+                    in_=x_rows[row][g * channels : (g + 1) * channels].rearrange("c j b v -> c j (b v)"),
                 )
 
         def quantise_patches(pair):
+            s = pair % PAIRS_IN_ROW
             patch_codes[pair] = patch_mx_pool.tile([P, CHUNKS * P], U32, name="patch_codes", align_bytes=64)
             patch_scales[pair] = patch_mx_pool.tile([P, CHUNKS * P], U8, name="patch_scales", align_bytes=64)
             nc.vector.quantize_mx(
                 out=patch_codes[pair][:].bitcast(FP8X4),
                 scales=patch_scales[pair][:],
-                in_=patches[pair][:].rearrange("p t g b v -> p (t g b v)"),
+                in_=ring[:, PAIR * s : PAIR * (s + 1), :, :].rearrange("p j g n -> p (j g n)"),
             )
 
         def multiply(pair):
@@ -169,27 +201,35 @@ def tile_stdpconvinhibit_kernel(tc, in_spikes, weights, out):
         def exists(pair):
             return 0 <= pair < PAIRS
 
+        def unit(step):
+            return WIN + step // PAIRS_IN_ROW, step % PAIRS_IN_ROW
+
+        units = (IMG - WIN) * PAIRS_IN_ROW
+
         make_identity(nc, identity[:])
         load_image()
+        for g in range(PASSES):
+            first_window(g)
         for step in range(-4, PAIRS + 1):
             if exists(step + 4):
                 load_weights(step + 4)
             if exists(step - 1):
                 multiply(step - 1)
-            if exists(step + 1):
-                quantise_patches(step + 1)
-            if exists(step + 3):
-                if step + 3 == 0:
-                    fill_ring()
-                elif (step + 3) % PAIRS_IN_ROW == 0:
-                    turn_ring((step + 3) // PAIRS_IN_ROW)
-                transpose_words(step + 3)
-            if exists(step + 2):
-                copy_out_patches(step + 2)
+            if 0 <= step + 4 < units and (step + 4) % PAIRS_IN_ROW == 0:
+                align_row(unit(step + 4)[0])
+            if 0 <= step + 3 < units:
+                transpose_row(unit(step + 3)[0], unit(step + 3)[1])
+            if 0 <= step + 2 < units:
+                copy_out_row(unit(step + 2)[0], unit(step + 2)[1])
+                if unit(step + 2)[1] == PAIRS_IN_ROW - 1:
+                    spread_row(unit(step + 2)[0])
             if exists(step):
                 quantise_weights(step)
             if exists(step + 1):
                 regroup_weights(step + 1)
+            if exists(step + 1) and (step + 1) % PAIRS_IN_ROW == 0:
+                for s in range(PAIRS_IN_ROW):
+                    quantise_patches(step + 1 + s)
             if exists(step - 1) and (step - 1) % 2 == 1:
                 copy_out_result((step - 1) // 2)
 

@@ -131,11 +131,11 @@ def tile_stdpconvinhibit_kernel(tc, in_spikes, weights, out):
                     planes[g, s][:].rearrange("p t h b -> p t b h"),
                 )
 
-        def align_row(row):
+        def align_rows():
             for first in range(2):
                 nc.vector.tensor_copy(
-                    out=rows[:, row - WIN, first, :, :],
-                    in_=image[:, :, row, first : first + ROW_COLS],
+                    out=rows[:, :, first, :, :],
+                    in_=image[:, :, WIN:IMG, first : first + ROW_COLS].rearrange("b c r w -> b r c w"),
                 )
 
         def transpose_row(row, s):
@@ -210,13 +210,12 @@ def tile_stdpconvinhibit_kernel(tc, in_spikes, weights, out):
         load_image()
         for g in range(PASSES):
             first_window(g)
+        align_rows()
         for step in range(-4, PAIRS + 1):
             if exists(step + 4):
                 load_weights(step + 4)
             if exists(step - 1):
                 multiply(step - 1)
-            if 0 <= step + 4 < units and (step + 4) % PAIRS_IN_ROW == 0:
-                align_row(unit(step + 4)[0])
             if 0 <= step + 3 < units:
                 transpose_row(unit(step + 3)[0], unit(step + 3)[1])
             if 0 <= step + 2 < units:

@@ -222,10 +222,10 @@ def tile_stdpconvinhibit_kernel(tc, in_spikes, weights, out):
                 copy_out_row(unit(step + 2)[0], unit(step + 2)[1])
                 if unit(step + 2)[1] == PAIRS_IN_ROW - 1:
                     spread_row(unit(step + 2)[0])
-            if exists(step):
-                quantise_weights(step)
             if exists(step + 1):
                 regroup_weights(step + 1)
+            if exists(step):
+                quantise_weights(step)
             if exists(step + 1) and (step + 1) % PAIRS_IN_ROW == 0:
                 for s in range(PAIRS_IN_ROW):
                     quantise_patches(step + 1 + s)

@@ -134,8 +134,8 @@ def tile_stdpconvinhibit_kernel(tc, in_spikes, weights, out):
         def align_rows():
             for first in range(2):
                 nc.vector.tensor_copy(
-                    out=rows[:, :, first, :, :],
-                    in_=image[:, :, WIN:IMG, first : first + ROW_COLS].rearrange("b c r w -> b r c w"),
+                    out=rows[:, :, first, :, :].rearrange("b r (c g) w -> b r c g w", g=PASSES),
+                    in_=image[:, :, WIN:IMG, first : first + ROW_COLS].rearrange("b (g c) r w -> b r c g w", g=PASSES),
                 )
 
         def transpose_row(row, s):
@@ -162,7 +162,7 @@ def tile_stdpconvinhibit_kernel(tc, in_spikes, weights, out):
             for g in range(PASSES):
                 nc.sync.dma_start(
                     out=ring[row % WIN : P : WIN, :, g, :],
-                    in_=x_rows[row][g * channels : (g + 1) * channels].rearrange("c j b v -> c j (b v)"),
+                    in_=x_rows[row][g:P:PASSES].rearrange("c j b v -> c j (b v)"),
                 )
 
         def quantise_patches(pair):

@@ -58,12 +58,12 @@ def tile_stdpconvinhibit_kernel(tc, in_spikes, weights, out):
             .bitcast(F32)
             .rearrange("b (r f c a) -> b r f c a", r=IMG - WIN, f=2, a=ROW_WORDS)
         )
-        ring = keep.tile([P, OUT, PASSES, P * WIN], BF16, name="ring", align_bytes=64)
+        ring = keep.tile([P, PAIRS_IN_ROW, PASSES, PAIR, P * WIN], BF16, name="ring", align_bytes=64)
         ring_words = (
             ring[:]
-            .rearrange("p j g n -> p (j g n)")
+            .rearrange("p s g t n -> p (s g t n)")
             .bitcast(F32)
-            .rearrange("p (j g b h) -> p j g b h", j=OUT, g=PASSES, h=2)
+            .rearrange("p (s g t b h) -> p s g t b h", s=PAIRS_IN_ROW, g=PASSES, t=PAIR, h=2)
         )
         w_raw, w_grouped, w_codes, w_scales = {}, {}, {}, {}
         planes, x_rows, x_words, patch_codes, patch_scales, acc = {}, {}, {}, {}, {}, {}
@@ -127,7 +127,7 @@ def tile_stdpconvinhibit_kernel(tc, in_spikes, weights, out):
             for s in range(PAIRS_IN_ROW):
                 copy_words(
                     s == 9,
-                    ring_words[:, PAIR * s : PAIR * (s + 1), g, :, :],
+                    ring_words[:, s, g, :, :, :],
                     planes[g, s][:].rearrange("p t h b -> p t b h"),
                 )
 
@@ -161,8 +161,8 @@ def tile_stdpconvinhibit_kernel(tc, in_spikes, weights, out):
         def spread_row(row):
             for g in range(PASSES):
                 nc.sync.dma_start(
-                    out=ring[row % WIN : P : WIN, :, g, :],
-                    in_=x_rows[row][g:P:PASSES].rearrange("c j b v -> c j (b v)"),
+                    out=ring[row % WIN : P : WIN, :, g, :, :].rearrange("p s t n -> p s (t n)"),
+                    in_=x_rows[row][g:P:PASSES].rearrange("c (s t) b v -> c s (t b v)", t=PAIR),
                 )
 
         def quantise_patches(pair):
@@ -172,7 +172,7 @@ def tile_stdpconvinhibit_kernel(tc, in_spikes, weights, out):
             nc.vector.quantize_mx(
                 out=patch_codes[pair][:].bitcast(FP8X4),
                 scales=patch_scales[pair][:],
-                in_=ring[:, PAIR * s : PAIR * (s + 1), :, :].rearrange("p j g n -> p (j g n)"),
+                in_=ring[:, s, :, :, :].rearrange("p g t n -> p (g t n)"),
             )
 
         def multiply(pair):
@@ -182,10 +182,11 @@ def tile_stdpconvinhibit_kernel(tc, in_spikes, weights, out):
             for t in range(PAIR):
                 for g in range(PASSES):
                     cols = slice((t * PASSES + g) * P, (t * PASSES + g + 1) * P)
+                    patch_cols = slice((g * PAIR + t) * P, (g * PAIR + t + 1) * P)
                     nc.tensor.matmul_mx(
                         out=acc[bank][:, (pair % 2) * PAIR + t, :],
-                        lhsT=patch_codes[pair][:, cols].bitcast(FP8X4),
-                        lhsT_scale=patch_scales[pair][:, cols],
+                        lhsT=patch_codes[pair][:, patch_cols].bitcast(FP8X4),
+                        lhsT_scale=patch_scales[pair][:, patch_cols],
                         rhs=w_codes[pair][:, cols].bitcast(FP8X4),
                         rhs_scale=w_scales[pair][:, cols],
                         start=(g == 0),

@@ -21,6 +21,7 @@ PAIRS = OUT * PAIRS_IN_ROW
 ROW_COLS = 8
 ROW_WORDS = ROW_COLS // 2
 K_SCALAR = 76
+PAIRS_BY_TENSOR = 7
 
 FLOPS = 2 * P * (P * WIN * WIN) * P * OUT * OUT
 
@@ -37,12 +38,14 @@ def tile_stdpconvinhibit_kernel(tc, in_spikes, weights, out):
         w_mx_pool = stack.enter_context(tc.tile_pool(name="w_mx", bufs=3))
         x_pool = stack.enter_context(tc.tile_pool(name="x", bufs=2))
         patch_mx_pool = stack.enter_context(tc.tile_pool(name="patch_mx", bufs=6))
-        planes_pool = stack.enter_context(tc.psum_pool(name="planes", bufs=6))
+        planes_pool = stack.enter_context(tc.psum_pool(name="planes", bufs=5))
+        w_bank_pool = stack.enter_context(tc.psum_pool(name="w_bank", bufs=1))
         acc_pool = stack.enter_context(tc.psum_pool(name="acc", bufs=2))
         stack.enter_context(tc.manual_schedule())
 
         image = keep.tile([P, P, IMG, IMG], BF16, name="image")
         identity = keep.tile([P, P], F32, name="identity")
+        identity_bf16 = keep.tile([P, P], BF16, name="identity_bf16")
         result = keep.tile([P, P, OUT * OUT], F32, name="result")
         top = keep.tile([P, 2, P * WIN, ROW_COLS], BF16, name="top")
         top_words = (
@@ -65,7 +68,7 @@ def tile_stdpconvinhibit_kernel(tc, in_spikes, weights, out):
             .bitcast(F32)
             .rearrange("p (s g t b h) -> p s g t b h", s=PAIRS_IN_ROW, g=PASSES, t=PAIR, h=2)
         )
-        w_raw, w_grouped, w_codes, w_scales = {}, {}, {}, {}
+        w_raw, w_grouped, w_codes, w_scales, w_bank = {}, {}, {}, {}, {}
         planes, x_rows, x_words, patch_codes, patch_scales, acc = {}, {}, {}, {}, {}, {}
 
         def load_image():
@@ -86,15 +89,36 @@ def tile_stdpconvinhibit_kernel(tc, in_spikes, weights, out):
                     in_=w_view[u, :, pair * CHUNKS : (pair + 1) * CHUNKS, :],
                 )
 
+        def by_tensor(pair):
+            return pair % 2 == 1 and pair < 2 * PAIRS_BY_TENSOR
+
+        def regroup_by_tensor(pair):
+            w_bank[pair] = w_bank_pool.tile([P, 2, P * WIN], BF16, name="w_bank")
+            for n in range(2):
+                nc.tensor.matmul(
+                    out=w_bank[pair][:, n, :],
+                    lhsT=identity_bf16[:],
+                    rhs=w_raw[pair][:, CHUNKS - 2 + n, :, :].rearrange("p v k -> p k v"),
+                    start=True,
+                    stop=True,
+                )
+
         def regroup_weights(pair):
             w_grouped[pair] = w_grouped_pool.tile([P, CHUNKS, P, WIN], BF16, name="w_grouped", align_bytes=64)
+            direct = CHUNKS
+            if by_tensor(pair):
+                direct = CHUNKS - 2
+                nc.scalar.copy(
+                    out=w_grouped[pair][:, direct:CHUNKS, :, :].rearrange("p n k v -> p n (k v)"),
+                    in_=w_bank[pair][:],
+                )
             nc.scalar.copy(
-                out=w_grouped[pair][:, :, 0:K_SCALAR, :].rearrange("p n (q r) v -> p n q v r", r=4),
-                in_=w_raw[pair][:, :, :, 0:K_SCALAR].rearrange("p n v (q r) -> p n q v r", r=4),
+                out=w_grouped[pair][:, 0:direct, 0:K_SCALAR, :].rearrange("p n (q r) v -> p n q v r", r=4),
+                in_=w_raw[pair][:, 0:direct, :, 0:K_SCALAR].rearrange("p n v (q r) -> p n q v r", r=4),
             )
             nc.vector.tensor_copy(
-                out=w_grouped[pair][:, :, K_SCALAR:P, :].rearrange("p n (q r) v -> p n q v r", r=4),
-                in_=w_raw[pair][:, :, :, K_SCALAR:P].rearrange("p n v (q r) -> p n q v r", r=4),
+                out=w_grouped[pair][:, 0:direct, K_SCALAR:P, :].rearrange("p n (q r) v -> p n q v r", r=4),
+                in_=w_raw[pair][:, 0:direct, :, K_SCALAR:P].rearrange("p n v (q r) -> p n q v r", r=4),
             )
 
         def quantise_weights(pair):
@@ -208,6 +232,7 @@ def tile_stdpconvinhibit_kernel(tc, in_spikes, weights, out):
         units = (IMG - WIN) * PAIRS_IN_ROW
 
         make_identity(nc, identity[:])
+        make_identity(nc, identity_bf16[:])
         load_image()
         for g in range(PASSES):
             first_window(g)
@@ -223,6 +248,8 @@ def tile_stdpconvinhibit_kernel(tc, in_spikes, weights, out):
                 copy_out_row(unit(step + 2)[0], unit(step + 2)[1])
                 if unit(step + 2)[1] == PAIRS_IN_ROW - 1:
                     spread_row(unit(step + 2)[0])
+            if exists(step + 2) and by_tensor(step + 2):
+                regroup_by_tensor(step + 2)
             if exists(step + 1):
                 regroup_weights(step + 1)
             if exists(step):

@@ -21,6 +21,8 @@ PAIRS = OUT * PAIRS_IN_ROW
 ROW_COLS = 8
 ROW_WORDS = ROW_COLS // 2
 K_SCALAR = 76
+K_SCALAR_LATE = 96
+FIRST_LATE_PAIR = 17
 PAIRS_BY_TENSOR = 7
 
 FLOPS = 2 * P * (P * WIN * WIN) * P * OUT * OUT
@@ -105,6 +107,7 @@ def tile_stdpconvinhibit_kernel(tc, in_spikes, weights, out):
 
         def regroup_weights(pair):
             w_grouped[pair] = w_grouped_pool.tile([P, CHUNKS, P, WIN], BF16, name="w_grouped", align_bytes=64)
+            k_scalar = K_SCALAR if pair < FIRST_LATE_PAIR else K_SCALAR_LATE
             direct = CHUNKS
             if by_tensor(pair):
                 direct = CHUNKS - 2
@@ -113,22 +116,26 @@ def tile_stdpconvinhibit_kernel(tc, in_spikes, weights, out):
                     in_=w_bank[pair][:],
                 )
             nc.scalar.copy(
-                out=w_grouped[pair][:, 0:direct, 0:K_SCALAR, :].rearrange("p n (q r) v -> p n q v r", r=4),
-                in_=w_raw[pair][:, 0:direct, :, 0:K_SCALAR].rearrange("p n v (q r) -> p n q v r", r=4),
+                out=w_grouped[pair][:, 0:direct, 0:k_scalar, :].rearrange("p n (q r) v -> p n q v r", r=4),
+                in_=w_raw[pair][:, 0:direct, :, 0:k_scalar].rearrange("p n v (q r) -> p n q v r", r=4),
             )
             nc.vector.tensor_copy(
-                out=w_grouped[pair][:, 0:direct, K_SCALAR:P, :].rearrange("p n (q r) v -> p n q v r", r=4),
-                in_=w_raw[pair][:, 0:direct, :, K_SCALAR:P].rearrange("p n v (q r) -> p n q v r", r=4),
+                out=w_grouped[pair][:, 0:direct, k_scalar:P, :].rearrange("p n (q r) v -> p n q v r", r=4),
+                in_=w_raw[pair][:, 0:direct, :, k_scalar:P].rearrange("p n v (q r) -> p n q v r", r=4),
             )
 
         def quantise_weights(pair):
             w_codes[pair] = w_mx_pool.tile([P, CHUNKS * P], U32, name="w_codes", align_bytes=64)
             w_scales[pair] = w_mx_pool.tile([P, CHUNKS * P], U8, name="w_scales", align_bytes=64)
-            nc.vector.quantize_mx(
-                out=w_codes[pair][:].bitcast(FP8X4),
-                scales=w_scales[pair][:],
-                in_=w_grouped[pair][:].rearrange("p n k v -> p (n k v)"),
-            )
+            parts = PAIR if pair == PAIRS - 1 else 1
+            width = CHUNKS * P // parts
+            for part in range(parts):
+                cols = slice(part * width, (part + 1) * width)
+                nc.vector.quantize_mx(
+                    out=w_codes[pair][:, cols].bitcast(FP8X4),
+                    scales=w_scales[pair][:, cols],
+                    in_=w_grouped[pair][:].rearrange("p n k v -> p (n k v)")[:, part * width * WIN : (part + 1) * width * WIN],
+                )
 
         def copy_words(on_vector, dst, src):
             if on_vector:
@@ -218,10 +225,19 @@ def tile_stdpconvinhibit_kernel(tc, in_spikes, weights, out):
                     )
 
         def copy_out_result(bank):
-            nc.scalar.copy(
-                out=result[:, :, bank * 2 * PAIR : (bank + 1) * 2 * PAIR],
-                in_=acc[bank][:].rearrange("b q k -> b k q"),
-            )
+            last = bank == PAIRS // 2 - 1
+            halves = 2 if last else 1
+            for half in range(halves):
+                some = slice(half * P // halves, (half + 1) * P // halves)
+                nc.scalar.copy(
+                    out=result[:, some, bank * 2 * PAIR : (bank + 1) * 2 * PAIR],
+                    in_=acc[bank][:, :, some].rearrange("b q k -> b k q"),
+                )
+                if last:
+                    nc.sync.dma_start(
+                        out=out[:, some].rearrange("b k i j -> b (k i j)"),
+                        in_=result[:, some, :].rearrange("b k q -> b (k q)"),
+                    )
 
         def exists(pair):
             return 0 <= pair < PAIRS
@@ -259,8 +275,3 @@ def tile_stdpconvinhibit_kernel(tc, in_spikes, weights, out):
                     quantise_patches(step + 1 + s)
             if exists(step - 1) and (step - 1) % 2 == 1:
                 copy_out_result((step - 1) // 2)
-
-        nc.sync.dma_start(
-            out=out.rearrange("b k i j -> b (k i j)"),
-            in_=result[:].rearrange("b k q -> b (k q)"),
-        )

@@ -20,7 +20,7 @@ PAIRS_IN_ROW = OUT // PAIR
 PAIRS = OUT * PAIRS_IN_ROW
 ROW_COLS = 8
 ROW_WORDS = ROW_COLS // 2
-K_SCALAR = 76
+K_SCALAR = 68
 K_SCALAR_LATE = 96
 FIRST_LATE_PAIR = 17
 PAIRS_BY_TENSOR = 7

@@ -31,6 +31,7 @@ FLOPS = 2 * P * (P * WIN * WIN) * P * OUT * OUT
 def tile_stdpconvinhibit_kernel(tc, in_spikes, weights, out):
     nc = tc.nc
     w_view = weights.rearrange("i j (g c) u v k -> u c (i j g) (v k)", g=PASSES)
+    w_rows = weights.rearrange("i j (g c) u v k -> (c u) (i j g) (v k)", g=PASSES)
     channels = P // PASSES
 
     with ExitStack() as stack:
@@ -84,6 +85,12 @@ def tile_stdpconvinhibit_kernel(tc, in_spikes, weights, out):
         def load_weights(pair):
             i = pair // PAIRS_IN_ROW
             w_raw[pair] = w_raw_pool.tile([P, CHUNKS, WIN, P], BF16, name="w_raw")
+            if i % WIN == 0:
+                nc.sync.dma_start(
+                    out=w_raw[pair][:].rearrange("p n v k -> p n (v k)"),
+                    in_=w_rows[:, pair * CHUNKS : (pair + 1) * CHUNKS, :],
+                )
+                return
             for u in range(WIN):
                 r = (i + u) % WIN
                 nc.sync.dma_start(

@@ -20,11 +20,18 @@ PAIRS_IN_ROW = OUT // PAIR
 PAIRS = OUT * PAIRS_IN_ROW
 ROW_COLS = 8
 ROW_WORDS = ROW_COLS // 2
-K_SCALAR = 68
-K_SCALAR_LATE = 96
-FIRST_LATE_PAIR = 17
+K_SCALAR_FIRST = 60
+FIRST_PAIRS = 4
+K_SCALAR = 72
+K_SCALAR_HALF = 36
+HALF = P // 2
+FULL_PAIRS = PAIRS - 2
+JOBS = [(pair, 0, P) for pair in range(FULL_PAIRS)] + [(pair, k0, k0 + HALF) for k0 in (0, HALF) for pair in range(FULL_PAIRS, PAIRS)]
 PAIRS_BY_TENSOR = 7
 
+F0 = FULL_PAIRS
+SCALAR_HALVES = {F0 - 1: [F0, F0 + 2], F0: [F0 + 1], F0 + 1: [F0 + 3]}
+VECTOR_HALVES = {F0 - 1: [F0], F0: [F0 + 1], F0 + 2: [F0 + 2, F0 + 3]}
 FLOPS = 2 * P * (P * WIN * WIN) * P * OUT * OUT
 
 
@@ -36,8 +43,9 @@ def tile_stdpconvinhibit_kernel(tc, in_spikes, weights, out):
 
     with ExitStack() as stack:
         keep = stack.enter_context(tc.tile_pool(name="keep", bufs=1))
-        w_raw_pool = stack.enter_context(tc.tile_pool(name="w_raw", bufs=4))
+        w_raw_pool = stack.enter_context(tc.tile_pool(name="w_raw", bufs=5))
         w_grouped_pool = stack.enter_context(tc.tile_pool(name="w_grouped", bufs=3))
+        w_half_pool = stack.enter_context(tc.tile_pool(name="w_half", bufs=4))
         w_mx_pool = stack.enter_context(tc.tile_pool(name="w_mx", bufs=3))
         x_pool = stack.enter_context(tc.tile_pool(name="x", bufs=2))
         patch_mx_pool = stack.enter_context(tc.tile_pool(name="patch_mx", bufs=6))
@@ -82,21 +90,26 @@ def tile_stdpconvinhibit_kernel(tc, in_spikes, weights, out):
                     in_=in_spikes[:, some].rearrange("b c h w -> b (c h w)"),
                 )
 
-        def load_weights(pair):
-            i = pair // PAIRS_IN_ROW
-            w_raw[pair] = w_raw_pool.tile([P, CHUNKS, WIN, P], BF16, name="w_raw")
-            if i % WIN == 0:
-                nc.sync.dma_start(
-                    out=w_raw[pair][:].rearrange("p n v k -> p n (v k)"),
-                    in_=w_rows[:, pair * CHUNKS : (pair + 1) * CHUNKS, :],
-                )
-                return
-            for u in range(WIN):
-                r = (i + u) % WIN
-                nc.sync.dma_start(
-                    out=w_raw[pair][r:P:WIN].rearrange("p n v k -> p n (v k)"),
-                    in_=w_view[u, :, pair * CHUNKS : (pair + 1) * CHUNKS, :],
-                )
+        loads = [(pair, u) for pair in range(PAIRS) for u in range(WIN)]
+        issued = []
+
+        def load_weights(count):
+            while len(issued) < min(count, len(loads)):
+                pair, u = loads[len(issued)]
+                issued.append(pair)
+                i = pair // PAIRS_IN_ROW
+                if u == 0:
+                    w_raw[pair] = w_raw_pool.tile([P, CHUNKS, WIN, P], BF16, name="w_raw")
+                    if i == 0:
+                        nc.sync.dma_start(
+                            out=w_raw[pair][:].rearrange("p n v k -> p n (v k)"),
+                            in_=w_rows[:, pair * CHUNKS : (pair + 1) * CHUNKS, :],
+                        )
+                if i > 0:
+                    nc.sync.dma_start(
+                        out=w_raw[pair][(i + u) % WIN : P : WIN].rearrange("p n v k -> p n (v k)"),
+                        in_=w_view[u, :, pair * CHUNKS : (pair + 1) * CHUNKS, :],
+                    )
 
         def by_tensor(pair):
             return pair % 2 == 1 and pair < 2 * PAIRS_BY_TENSOR
@@ -112,37 +125,46 @@ def tile_stdpconvinhibit_kernel(tc, in_spikes, weights, out):
                     stop=True,
                 )
 
-        def regroup_weights(pair):
-            w_grouped[pair] = w_grouped_pool.tile([P, CHUNKS, P, WIN], BF16, name="w_grouped", align_bytes=64)
-            k_scalar = K_SCALAR if pair < FIRST_LATE_PAIR else K_SCALAR_LATE
+        def regroup_weights(job, on_scalar, on_vector):
+            pair, k0, k1 = JOBS[job]
+            if job in w_grouped:
+                pass
+            elif k1 - k0 == P:
+                w_grouped[job] = w_grouped_pool.tile([P, CHUNKS, P, WIN], BF16, name="w_grouped", align_bytes=64)
+            else:
+                w_grouped[job] = w_half_pool.tile([P, CHUNKS, HALF, WIN], BF16, name="w_half", align_bytes=64)
+            if k1 - k0 < P:
+                k_scalar = K_SCALAR_HALF
+            else:
+                k_scalar = K_SCALAR_FIRST if pair < FIRST_PAIRS else K_SCALAR
             direct = CHUNKS
             if by_tensor(pair):
                 direct = CHUNKS - 2
+            if by_tensor(pair) and on_scalar:
                 nc.scalar.copy(
-                    out=w_grouped[pair][:, direct:CHUNKS, :, :].rearrange("p n k v -> p n (k v)"),
+                    out=w_grouped[job][:, direct:CHUNKS, :, :].rearrange("p n k v -> p n (k v)"),
                     in_=w_bank[pair][:],
                 )
-            nc.scalar.copy(
-                out=w_grouped[pair][:, 0:direct, 0:k_scalar, :].rearrange("p n (q r) v -> p n q v r", r=4),
-                in_=w_raw[pair][:, 0:direct, :, 0:k_scalar].rearrange("p n v (q r) -> p n q v r", r=4),
+            if on_scalar:
+              nc.scalar.copy(
+                out=w_grouped[job][:, 0:direct, 0:k_scalar, :].rearrange("p n (q r) v -> p n q v r", r=4),
+                in_=w_raw[pair][:, 0:direct, :, k0 : k0 + k_scalar].rearrange("p n v (q r) -> p n q v r", r=4),
             )
-            nc.vector.tensor_copy(
-                out=w_grouped[pair][:, 0:direct, k_scalar:P, :].rearrange("p n (q r) v -> p n q v r", r=4),
-                in_=w_raw[pair][:, 0:direct, :, k_scalar:P].rearrange("p n v (q r) -> p n q v r", r=4),
+            if on_vector:
+              nc.vector.tensor_copy(
+                out=w_grouped[job][:, 0:direct, k_scalar:, :].rearrange("p n (q r) v -> p n q v r", r=4),
+                in_=w_raw[pair][:, 0:direct, :, k0 + k_scalar : k1].rearrange("p n v (q r) -> p n q v r", r=4),
             )
 
-        def quantise_weights(pair):
-            w_codes[pair] = w_mx_pool.tile([P, CHUNKS * P], U32, name="w_codes", align_bytes=64)
-            w_scales[pair] = w_mx_pool.tile([P, CHUNKS * P], U8, name="w_scales", align_bytes=64)
-            parts = PAIR if pair == PAIRS - 1 else 1
-            width = CHUNKS * P // parts
-            for part in range(parts):
-                cols = slice(part * width, (part + 1) * width)
-                nc.vector.quantize_mx(
-                    out=w_codes[pair][:, cols].bitcast(FP8X4),
-                    scales=w_scales[pair][:, cols],
-                    in_=w_grouped[pair][:].rearrange("p n k v -> p (n k v)")[:, part * width * WIN : (part + 1) * width * WIN],
-                )
+        def quantise_weights(job):
+            width = CHUNKS * (JOBS[job][2] - JOBS[job][1])
+            w_codes[job] = w_mx_pool.tile([P, width], U32, name="w_codes", align_bytes=64)
+            w_scales[job] = w_mx_pool.tile([P, width], U8, name="w_scales", align_bytes=64)
+            nc.vector.quantize_mx(
+                out=w_codes[job][:].bitcast(FP8X4),
+                scales=w_scales[job][:],
+                in_=w_grouped[job][:].rearrange("p n k v -> p (n k v)"),
+            )
 
         def copy_words(on_vector, dst, src):
             if on_vector:
@@ -213,38 +235,48 @@ def tile_stdpconvinhibit_kernel(tc, in_spikes, weights, out):
                 in_=ring[:, s, :, :, :].rearrange("p g t n -> p (g t n)"),
             )
 
-        def multiply(pair):
-            bank = pair // 2
+        def multiply(job):
+            pair, k0, k1 = JOBS[job]
+            bank = pair // 2 + (1 if k0 > 0 else 0)
             if pair % 2 == 0:
                 acc[bank] = acc_pool.tile([P, 2 * PAIR, P], F32, name="acc")
             for t in range(PAIR):
                 for g in range(PASSES):
-                    cols = slice((t * PASSES + g) * P, (t * PASSES + g + 1) * P)
+                    first = (t * PASSES + g) * (k1 - k0)
+                    if k1 - k0 == HALF and t == 1:
+                        first -= HALF
+                    cols = slice(first, first + P)
                     patch_cols = slice((g * PAIR + t) * P, (g * PAIR + t + 1) * P)
                     nc.tensor.matmul_mx(
                         out=acc[bank][:, (pair % 2) * PAIR + t, :],
                         lhsT=patch_codes[pair][:, patch_cols].bitcast(FP8X4),
                         lhsT_scale=patch_scales[pair][:, patch_cols],
-                        rhs=w_codes[pair][:, cols].bitcast(FP8X4),
-                        rhs_scale=w_scales[pair][:, cols],
+                        rhs=w_codes[job][:, cols].bitcast(FP8X4),
+                        rhs_scale=w_scales[job][:, cols],
                         start=(g == 0),
                         stop=(g == PASSES - 1),
                     )
 
-        def copy_out_result(bank):
-            last = bank == PAIRS // 2 - 1
-            halves = 2 if last else 1
-            for half in range(halves):
-                some = slice(half * P // halves, (half + 1) * P // halves)
+        def copy_out_result(job):
+            pair, k0, k1 = JOBS[job]
+            bank = pair // 2 + (1 if k0 > 0 else 0)
+            first = (pair - 1) * PAIR
+            if k1 - k0 == P:
                 nc.scalar.copy(
-                    out=result[:, some, bank * 2 * PAIR : (bank + 1) * 2 * PAIR],
-                    in_=acc[bank][:, :, some].rearrange("b q k -> b k q"),
+                    out=result[:, :, first : first + 2 * PAIR],
+                    in_=acc[bank][:].rearrange("b q k -> b k q"),
                 )
-                if last:
-                    nc.sync.dma_start(
-                        out=out[:, some].rearrange("b k i j -> b (k i j)"),
-                        in_=result[:, some, :].rearrange("b k q -> b (k q)"),
-                    )
+            else:
+                nc.scalar.copy(
+                    out=result[:, k0:k1, first : first + 2 * PAIR].rearrange("b k (r t) -> b k r t", t=PAIR),
+                    in_=acc[bank][:]
+                    .rearrange("b (r t) (h k) -> b r (t h) k", t=PAIR, h=2)[:, :, 0:4:3, :]
+                    .rearrange("b r t k -> b k r t"),
+                )
+                nc.sync.dma_start(
+                    out=out[:, k0:k1].rearrange("b k i j -> b (k i j)"),
+                    in_=result[:, k0:k1, :].rearrange("b k q -> b (k q)"),
+                )
 
         def exists(pair):
             return 0 <= pair < PAIRS
@@ -260,25 +292,29 @@ def tile_stdpconvinhibit_kernel(tc, in_spikes, weights, out):
         for g in range(PASSES):
             first_window(g)
         align_rows()
-        for step in range(-4, PAIRS + 1):
-            if exists(step + 4):
-                load_weights(step + 4)
-            if exists(step - 1):
+        for step in range(-4, len(JOBS) + 1):
+            load_weights(WIN * (step + 4 + 1))
+            if 0 <= step - 1:
                 multiply(step - 1)
+            if 0 <= step + 4 < units:
+                transpose_row(unit(step + 4)[0], unit(step + 4)[1])
             if 0 <= step + 3 < units:
-                transpose_row(unit(step + 3)[0], unit(step + 3)[1])
-            if 0 <= step + 2 < units:
-                copy_out_row(unit(step + 2)[0], unit(step + 2)[1])
-                if unit(step + 2)[1] == PAIRS_IN_ROW - 1:
-                    spread_row(unit(step + 2)[0])
+                copy_out_row(unit(step + 3)[0], unit(step + 3)[1])
             if exists(step + 2) and by_tensor(step + 2):
                 regroup_by_tensor(step + 2)
-            if exists(step + 1):
-                regroup_weights(step + 1)
-            if exists(step):
+            if 0 <= step + 1 < FULL_PAIRS:
+                regroup_weights(step + 1, True, True)
+            for job in SCALAR_HALVES.get(step, []):
+                regroup_weights(job, True, False)
+            for job in VECTOR_HALVES.get(step, []):
+                regroup_weights(job, False, True)
+            if 0 <= step < len(JOBS):
                 quantise_weights(step)
             if exists(step + 1) and (step + 1) % PAIRS_IN_ROW == 0:
                 for s in range(PAIRS_IN_ROW):
                     quantise_patches(step + 1 + s)
-            if exists(step - 1) and (step - 1) % 2 == 1:
-                copy_out_result((step - 1) // 2)
+            if 0 <= step + 3 < units and unit(step + 3)[1] == PAIRS_IN_ROW - 1:
+                load_weights(WIN * (step + 4 + 1) + 1)
+                spread_row(unit(step + 3)[0])
+            if 0 <= step - 1 and JOBS[step - 1][0] % 2 == 1:
+                copy_out_result(step - 1)

@@ -23,6 +23,8 @@ ROW_WORDS = ROW_COLS // 2
 K_SCALAR_FIRST = 60
 FIRST_PAIRS = 4
 K_SCALAR = 72
+FIRST_LATE_PAIR = 13
+K_SCALAR_LATE = 84
 K_SCALAR_HALF = 36
 HALF = P // 2
 FULL_PAIRS = PAIRS - 2
@@ -30,7 +32,7 @@ JOBS = [(pair, 0, P) for pair in range(FULL_PAIRS)] + [(pair, k0, k0 + HALF) for
 PAIRS_BY_TENSOR = 7
 
 F0 = FULL_PAIRS
-SCALAR_HALVES = {F0 - 1: [F0, F0 + 2], F0: [F0 + 1], F0 + 1: [F0 + 3]}
+SCALAR_HALVES = {F0 - 1: [F0, F0 + 2], F0: [F0 + 1, F0 + 3]}
 VECTOR_HALVES = {F0 - 1: [F0], F0: [F0 + 1], F0 + 2: [F0 + 2, F0 + 3]}
 FLOPS = 2 * P * (P * WIN * WIN) * P * OUT * OUT
 
@@ -136,7 +138,7 @@ def tile_stdpconvinhibit_kernel(tc, in_spikes, weights, out):
             if k1 - k0 < P:
                 k_scalar = K_SCALAR_HALF
             else:
-                k_scalar = K_SCALAR_FIRST if pair < FIRST_PAIRS else K_SCALAR
+                k_scalar = K_SCALAR_FIRST if pair < FIRST_PAIRS else K_SCALAR if pair < FIRST_LATE_PAIR else K_SCALAR_LATE
             direct = CHUNKS
             if by_tensor(pair):
                 direct = CHUNKS - 2
@@ -166,12 +168,6 @@ def tile_stdpconvinhibit_kernel(tc, in_spikes, weights, out):
                 in_=w_grouped[job][:].rearrange("p n k v -> p (n k v)"),
             )
 
-        def copy_words(on_vector, dst, src):
-            if on_vector:
-                nc.vector.tensor_copy(out=dst, in_=src)
-            else:
-                nc.scalar.copy(out=dst, in_=src)
-
         def first_window(g):
             some = slice(g * channels, (g + 1) * channels)
             for first in range(2):
@@ -179,23 +175,20 @@ def tile_stdpconvinhibit_kernel(tc, in_spikes, weights, out):
                     out=top[:, first, g * P : (g + 1) * P, :].rearrange("b (c r) w -> b c r w", r=WIN),
                     in_=image[:, some, 0:WIN, first : first + ROW_COLS],
                 )
+            for first in range(2):
+                nc.vector.tensor_copy(
+                    out=rows[:, :, first, g:P:PASSES, :],
+                    in_=image[:, some, WIN:IMG, first : first + ROW_COLS].rearrange("b c r w -> b r c w"),
+                )
             for s in range(PAIRS_IN_ROW):
                 planes[g, s] = planes_pool.tile([P, PAIR, 2, P], F32, name="planes")
                 for t in range(PAIR):
                     for h in range(2):
                         nc.tensor.transpose(planes[g, s][:, t, h, :], top_words[:, t, g * P : (g + 1) * P, s + h], identity[:])
             for s in range(PAIRS_IN_ROW):
-                copy_words(
-                    s == 9,
-                    ring_words[:, s, g, :, :, :],
-                    planes[g, s][:].rearrange("p t h b -> p t b h"),
-                )
-
-        def align_rows():
-            for first in range(2):
-                nc.vector.tensor_copy(
-                    out=rows[:, :, first, :, :].rearrange("b r (c g) w -> b r c g w", g=PASSES),
-                    in_=image[:, :, WIN:IMG, first : first + ROW_COLS].rearrange("b (g c) r w -> b r c g w", g=PASSES),
+                nc.scalar.copy(
+                    out=ring_words[:, s, g, :, :, :],
+                    in_=planes[g, s][:].rearrange("p t h b -> p t b h"),
                 )
 
         def transpose_row(row, s):
@@ -291,7 +284,6 @@ def tile_stdpconvinhibit_kernel(tc, in_spikes, weights, out):
         load_image()
         for g in range(PASSES):
             first_window(g)
-        align_rows()
         for step in range(-4, len(JOBS) + 1):
             load_weights(WIN * (step + 4 + 1))
             if 0 <= step - 1:

@@ -20,12 +20,12 @@ PAIRS_IN_ROW = OUT // PAIR
 PAIRS = OUT * PAIRS_IN_ROW
 ROW_COLS = 8
 ROW_WORDS = ROW_COLS // 2
-K_SCALAR_FIRST = 60
+K_SCALAR_FIRST = 52
 FIRST_PAIRS = 4
-K_SCALAR = 72
+K_SCALAR = 64
 FIRST_LATE_PAIR = 13
-K_SCALAR_LATE = 84
-K_SCALAR_HALF = 36
+K_SCALAR_LATE = 76
+K_SCALAR_HALF = 32
 HALF = P // 2
 FULL_PAIRS = PAIRS - 2
 JOBS = [(pair, 0, P) for pair in range(FULL_PAIRS)] + [(pair, k0, k0 + HALF) for k0 in (0, HALF) for pair in range(FULL_PAIRS, PAIRS)]

@@ -50,7 +50,7 @@ def tile_stdpconvinhibit_kernel(tc, in_spikes, weights, out):
         w_half_pool = stack.enter_context(tc.tile_pool(name="w_half", bufs=4))
         w_mx_pool = stack.enter_context(tc.tile_pool(name="w_mx", bufs=3))
         x_pool = stack.enter_context(tc.tile_pool(name="x", bufs=2))
-        patch_mx_pool = stack.enter_context(tc.tile_pool(name="patch_mx", bufs=6))
+        patch_mx_pool = stack.enter_context(tc.tile_pool(name="patch_mx", bufs=2))
         planes_pool = stack.enter_context(tc.psum_pool(name="planes", bufs=5))
         w_bank_pool = stack.enter_context(tc.psum_pool(name="w_bank", bufs=1))
         acc_pool = stack.enter_context(tc.psum_pool(name="acc", bufs=2))
@@ -74,12 +74,12 @@ def tile_stdpconvinhibit_kernel(tc, in_spikes, weights, out):
             .bitcast(F32)
             .rearrange("b (r f c a) -> b r f c a", r=IMG - WIN, f=2, a=ROW_WORDS)
         )
-        ring = keep.tile([P, PAIRS_IN_ROW, PASSES, PAIR, P * WIN], BF16, name="ring", align_bytes=64)
+        ring = keep.tile([P, PASSES, OUT, P * WIN], BF16, name="ring", align_bytes=64)
         ring_words = (
             ring[:]
-            .rearrange("p s g t n -> p (s g t n)")
+            .rearrange("p g j n -> p (g j n)")
             .bitcast(F32)
-            .rearrange("p (s g t b h) -> p s g t b h", s=PAIRS_IN_ROW, g=PASSES, t=PAIR, h=2)
+            .rearrange("p (g s t b h) -> p g s t b h", g=PASSES, s=PAIRS_IN_ROW, t=PAIR, h=2)
         )
         w_raw, w_grouped, w_codes, w_scales, w_bank = {}, {}, {}, {}, {}
         planes, x_rows, x_words, patch_codes, patch_scales, acc = {}, {}, {}, {}, {}, {}
@@ -102,12 +102,12 @@ def tile_stdpconvinhibit_kernel(tc, in_spikes, weights, out):
                 i = pair // PAIRS_IN_ROW
                 if u == 0:
                     w_raw[pair] = w_raw_pool.tile([P, CHUNKS, WIN, P], BF16, name="w_raw")
-                    if i == 0:
+                    if i % WIN == 0:
                         nc.sync.dma_start(
                             out=w_raw[pair][:].rearrange("p n v k -> p n (v k)"),
                             in_=w_rows[:, pair * CHUNKS : (pair + 1) * CHUNKS, :],
                         )
-                if i > 0:
+                if i % WIN > 0:
                     nc.sync.dma_start(
                         out=w_raw[pair][(i + u) % WIN : P : WIN].rearrange("p n v k -> p n (v k)"),
                         in_=w_view[u, :, pair * CHUNKS : (pair + 1) * CHUNKS, :],
@@ -162,11 +162,14 @@ def tile_stdpconvinhibit_kernel(tc, in_spikes, weights, out):
             width = CHUNKS * (JOBS[job][2] - JOBS[job][1])
             w_codes[job] = w_mx_pool.tile([P, width], U32, name="w_codes", align_bytes=64)
             w_scales[job] = w_mx_pool.tile([P, width], U8, name="w_scales", align_bytes=64)
-            nc.vector.quantize_mx(
-                out=w_codes[job][:].bitcast(FP8X4),
-                scales=w_scales[job][:],
-                in_=w_grouped[job][:].rearrange("p n k v -> p (n k v)"),
-            )
+            parts = PAIR if job == len(JOBS) - 1 else 1
+            for part in range(parts):
+                cols = slice(part * width // parts, (part + 1) * width // parts)
+                nc.vector.quantize_mx(
+                    out=w_codes[job][:, cols].bitcast(FP8X4),
+                    scales=w_scales[job][:, cols],
+                    in_=w_grouped[job][:].rearrange("p n k v -> p (n k v)")[:, cols.start * WIN : cols.stop * WIN],
+                )
 
         def first_window(g):
             some = slice(g * channels, (g + 1) * channels)
@@ -187,7 +190,7 @@ def tile_stdpconvinhibit_kernel(tc, in_spikes, weights, out):
                         nc.tensor.transpose(planes[g, s][:, t, h, :], top_words[:, t, g * P : (g + 1) * P, s + h], identity[:])
             for s in range(PAIRS_IN_ROW):
                 nc.scalar.copy(
-                    out=ring_words[:, s, g, :, :, :],
+                    out=ring_words[:, g, s, :, :, :],
                     in_=planes[g, s][:].rearrange("p t h b -> p t b h"),
                 )
 
@@ -214,19 +217,22 @@ def tile_stdpconvinhibit_kernel(tc, in_spikes, weights, out):
         def spread_row(row):
             for g in range(PASSES):
                 nc.sync.dma_start(
-                    out=ring[row % WIN : P : WIN, :, g, :, :].rearrange("p s t n -> p s (t n)"),
-                    in_=x_rows[row][g:P:PASSES].rearrange("c (s t) b v -> c s (t b v)", t=PAIR),
+                    out=ring[row % WIN : P : WIN, g, :, :].rearrange("p j n -> p (j n)"),
+                    in_=x_rows[row][g:P:PASSES].rearrange("c j b v -> c (j b v)"),
                 )
 
-        def quantise_patches(pair):
-            s = pair % PAIRS_IN_ROW
-            patch_codes[pair] = patch_mx_pool.tile([P, CHUNKS * P], U32, name="patch_codes", align_bytes=64)
-            patch_scales[pair] = patch_mx_pool.tile([P, CHUNKS * P], U8, name="patch_scales", align_bytes=64)
-            nc.vector.quantize_mx(
-                out=patch_codes[pair][:].bitcast(FP8X4),
-                scales=patch_scales[pair][:],
-                in_=ring[:, s, :, :, :].rearrange("p g t n -> p (g t n)"),
-            )
+        def quantise_patches(i, parts):
+            if 0 in parts:
+                patch_codes[i] = patch_mx_pool.tile([P, PASSES * OUT * P], U32, name="patch_codes", align_bytes=64)
+                patch_scales[i] = patch_mx_pool.tile([P, PASSES * OUT * P], U8, name="patch_scales", align_bytes=64)
+            width = CHUNKS * P
+            for part in parts:
+                cols = slice(part * width, (part + 1) * width)
+                nc.vector.quantize_mx(
+                    out=patch_codes[i][:, cols].bitcast(FP8X4),
+                    scales=patch_scales[i][:, cols],
+                    in_=ring[:].rearrange("p g j n -> p (g j n)")[:, cols.start * WIN : cols.stop * WIN],
+                )
 
         def multiply(job):
             pair, k0, k1 = JOBS[job]
@@ -239,11 +245,12 @@ def tile_stdpconvinhibit_kernel(tc, in_spikes, weights, out):
                     if k1 - k0 == HALF and t == 1:
                         first -= HALF
                     cols = slice(first, first + P)
-                    patch_cols = slice((g * PAIR + t) * P, (g * PAIR + t + 1) * P)
+                    chunk = g * OUT + pair % PAIRS_IN_ROW * PAIR + t
+                    patch_cols = slice(chunk * P, (chunk + 1) * P)
                     nc.tensor.matmul_mx(
                         out=acc[bank][:, (pair % 2) * PAIR + t, :],
-                        lhsT=patch_codes[pair][:, patch_cols].bitcast(FP8X4),
-                        lhsT_scale=patch_scales[pair][:, patch_cols],
+                        lhsT=patch_codes[pair // PAIRS_IN_ROW][:, patch_cols].bitcast(FP8X4),
+                        lhsT_scale=patch_scales[pair // PAIRS_IN_ROW][:, patch_cols],
                         rhs=w_codes[job][:, cols].bitcast(FP8X4),
                         rhs_scale=w_scales[job][:, cols],
                         start=(g == 0),
@@ -284,6 +291,7 @@ def tile_stdpconvinhibit_kernel(tc, in_spikes, weights, out):
         load_image()
         for g in range(PASSES):
             first_window(g)
+        quantise_patches(0, (0,))
         for step in range(-4, len(JOBS) + 1):
             load_weights(WIN * (step + 4 + 1))
             if 0 <= step - 1:
@@ -303,10 +311,9 @@ def tile_stdpconvinhibit_kernel(tc, in_spikes, weights, out):
             if 0 <= step < len(JOBS):
                 quantise_weights(step)
             if exists(step + 1) and (step + 1) % PAIRS_IN_ROW == 0:
-                for s in range(PAIRS_IN_ROW):
-                    quantise_patches(step + 1 + s)
+                quantise_patches((step + 1) // PAIRS_IN_ROW, (1, 2) if step < 0 else (0, 1, 2))
             if 0 <= step + 3 < units and unit(step + 3)[1] == PAIRS_IN_ROW - 1:
-                load_weights(WIN * (step + 4 + 1) + 1)
+                load_weights(WIN * (step + 4 + 1) + (1 if (step + 5) // PAIRS_IN_ROW % WIN > 0 else 0))
                 spread_row(unit(step + 3)[0])
             if 0 <= step - 1 and JOBS[step - 1][0] % 2 == 1:
                 copy_out_result(step - 1)

@@ -20,12 +20,12 @@ PAIRS_IN_ROW = OUT // PAIR
 PAIRS = OUT * PAIRS_IN_ROW
 ROW_COLS = 8
 ROW_WORDS = ROW_COLS // 2
-K_SCALAR_FIRST = 52
+K_SCALAR_FIRST = 48
 FIRST_PAIRS = 4
-K_SCALAR = 64
+K_SCALAR = 72
 FIRST_LATE_PAIR = 13
-K_SCALAR_LATE = 76
-K_SCALAR_HALF = 32
+K_SCALAR_LATE = 80
+K_SCALAR_HALVES = (64, 32, 16, 32)
 HALF = P // 2
 FULL_PAIRS = PAIRS - 2
 JOBS = [(pair, 0, P) for pair in range(FULL_PAIRS)] + [(pair, k0, k0 + HALF) for k0 in (0, HALF) for pair in range(FULL_PAIRS, PAIRS)]
@@ -136,7 +136,7 @@ def tile_stdpconvinhibit_kernel(tc, in_spikes, weights, out):
             else:
                 w_grouped[job] = w_half_pool.tile([P, CHUNKS, HALF, WIN], BF16, name="w_half", align_bytes=64)
             if k1 - k0 < P:
-                k_scalar = K_SCALAR_HALF
+                k_scalar = K_SCALAR_HALVES[job - F0]
             else:
                 k_scalar = K_SCALAR_FIRST if pair < FIRST_PAIRS else K_SCALAR if pair < FIRST_LATE_PAIR else K_SCALAR_LATE
             direct = CHUNKS
@@ -152,7 +152,7 @@ def tile_stdpconvinhibit_kernel(tc, in_spikes, weights, out):
                 out=w_grouped[job][:, 0:direct, 0:k_scalar, :].rearrange("p n (q r) v -> p n q v r", r=4),
                 in_=w_raw[pair][:, 0:direct, :, k0 : k0 + k_scalar].rearrange("p n v (q r) -> p n q v r", r=4),
             )
-            if on_vector:
+            if on_vector and k_scalar < k1 - k0:
               nc.vector.tensor_copy(
                 out=w_grouped[job][:, 0:direct, k_scalar:, :].rearrange("p n (q r) v -> p n q v r", r=4),
                 in_=w_raw[pair][:, 0:direct, :, k0 + k_scalar : k1].rearrange("p n v (q r) -> p n q v r", r=4),
@@ -162,14 +162,11 @@ def tile_stdpconvinhibit_kernel(tc, in_spikes, weights, out):
             width = CHUNKS * (JOBS[job][2] - JOBS[job][1])
             w_codes[job] = w_mx_pool.tile([P, width], U32, name="w_codes", align_bytes=64)
             w_scales[job] = w_mx_pool.tile([P, width], U8, name="w_scales", align_bytes=64)
-            parts = PAIR if job == len(JOBS) - 1 else 1
-            for part in range(parts):
-                cols = slice(part * width // parts, (part + 1) * width // parts)
-                nc.vector.quantize_mx(
-                    out=w_codes[job][:, cols].bitcast(FP8X4),
-                    scales=w_scales[job][:, cols],
-                    in_=w_grouped[job][:].rearrange("p n k v -> p (n k v)")[:, cols.start * WIN : cols.stop * WIN],
-                )
+            nc.vector.quantize_mx(
+                out=w_codes[job][:].bitcast(FP8X4),
+                scales=w_scales[job][:],
+                in_=w_grouped[job][:].rearrange("p n k v -> p (n k v)"),
+            )
 
         def first_window(g):
             some = slice(g * channels, (g + 1) * channels)

from contextlib import ExitStack

from concourse import mybir
from concourse.masks import make_identity

BF16 = mybir.dt.bfloat16
F32 = mybir.dt.float32
U32 = mybir.dt.uint32
U8 = mybir.dt.uint8
FP8X4 = mybir.dt.float8_e4m3fn_x4

P = 128
IMG = 9
OUT = 6
WIN = 4
PASSES = 4
PAIR = 2
CHUNKS = PAIR * PASSES
PAIRS_IN_ROW = OUT // PAIR
PAIRS = OUT * PAIRS_IN_ROW
ROW_COLS = 8
ROW_WORDS = ROW_COLS // 2
K_SCALAR_FIRST = 48
FIRST_PAIRS = 4
K_SCALAR = 72
FIRST_LATE_PAIR = 13
K_SCALAR_LATE = 80
K_SCALAR_HALVES = (64, 32, 16, 32)
HALF = P // 2
FULL_PAIRS = PAIRS - 2
JOBS = [(pair, 0, P) for pair in range(FULL_PAIRS)] + [(pair, k0, k0 + HALF) for k0 in (0, HALF) for pair in range(FULL_PAIRS, PAIRS)]
PAIRS_BY_TENSOR = 7

F0 = FULL_PAIRS
SCALAR_HALVES = {F0 - 1: [F0, F0 + 2], F0: [F0 + 1, F0 + 3]}
VECTOR_HALVES = {F0 - 1: [F0], F0: [F0 + 1], F0 + 2: [F0 + 2, F0 + 3]}
FLOPS = 2 * P * (P * WIN * WIN) * P * OUT * OUT


def tile_stdpconvinhibit_kernel(tc, in_spikes, weights, out):
    nc = tc.nc
    w_view = weights.rearrange("i j (g c) u v k -> u c (i j g) (v k)", g=PASSES)
    w_rows = weights.rearrange("i j (g c) u v k -> (c u) (i j g) (v k)", g=PASSES)
    channels = P // PASSES

    with ExitStack() as stack:
        keep = stack.enter_context(tc.tile_pool(name="keep", bufs=1))
        w_raw_pool = stack.enter_context(tc.tile_pool(name="w_raw", bufs=5))
        w_grouped_pool = stack.enter_context(tc.tile_pool(name="w_grouped", bufs=3))
        w_half_pool = stack.enter_context(tc.tile_pool(name="w_half", bufs=4))
        w_mx_pool = stack.enter_context(tc.tile_pool(name="w_mx", bufs=3))
        x_pool = stack.enter_context(tc.tile_pool(name="x", bufs=2))
        patch_mx_pool = stack.enter_context(tc.tile_pool(name="patch_mx", bufs=2))
        planes_pool = stack.enter_context(tc.psum_pool(name="planes", bufs=5))
        w_bank_pool = stack.enter_context(tc.psum_pool(name="w_bank", bufs=1))
        acc_pool = stack.enter_context(tc.psum_pool(name="acc", bufs=2))
        stack.enter_context(tc.manual_schedule())

        image = keep.tile([P, P, IMG, IMG], BF16, name="image")
        identity = keep.tile([P, P], F32, name="identity")
        identity_bf16 = keep.tile([P, P], BF16, name="identity_bf16")
        result = keep.tile([P, P, OUT * OUT], F32, name="result")
        top = keep.tile([P, 2, P * WIN, ROW_COLS], BF16, name="top")
        top_words = (
            top[:]
            .rearrange("b f m w -> b (f m w)")
            .bitcast(F32)
            .rearrange("b (f m a) -> b f m a", f=2, a=ROW_WORDS)
        )
        rows = keep.tile([P, IMG - WIN, 2, P, ROW_COLS], BF16, name="rows")
        rows_words = (
            rows[:]
            .rearrange("b r f c w -> b (r f c w)")
            .bitcast(F32)
            .rearrange("b (r f c a) -> b r f c a", r=IMG - WIN, f=2, a=ROW_WORDS)
        )
        ring = keep.tile([P, PASSES, OUT, P * WIN], BF16, name="ring", align_bytes=64)
        ring_words = (
            ring[:]
            .rearrange("p g j n -> p (g j n)")
            .bitcast(F32)
            .rearrange("p (g s t b h) -> p g s t b h", g=PASSES, s=PAIRS_IN_ROW, t=PAIR, h=2)
        )
        w_raw, w_grouped, w_codes, w_scales, w_bank = {}, {}, {}, {}, {}
        planes, x_rows, x_words, patch_codes, patch_scales, acc = {}, {}, {}, {}, {}, {}

        def load_image():
            for g in range(PASSES):
                some = slice(g * channels, (g + 1) * channels)
                nc.sync.dma_start(
                    out=image[:, some].rearrange("b c h w -> b (c h w)"),
                    in_=in_spikes[:, some].rearrange("b c h w -> b (c h w)"),
                )

        loads = [(pair, u) for pair in range(PAIRS) for u in range(WIN)]
        issued = []

        def load_weights(count):
            while len(issued) < min(count, len(loads)):
                pair, u = loads[len(issued)]
                issued.append(pair)
                i = pair // PAIRS_IN_ROW
                if u == 0:
                    w_raw[pair] = w_raw_pool.tile([P, CHUNKS, WIN, P], BF16, name="w_raw")
                    if i % WIN == 0:
                        nc.sync.dma_start(
                            out=w_raw[pair][:].rearrange("p n v k -> p n (v k)"),
                            in_=w_rows[:, pair * CHUNKS : (pair + 1) * CHUNKS, :],
                        )
                if i % WIN > 0:
                    nc.sync.dma_start(
                        out=w_raw[pair][(i + u) % WIN : P : WIN].rearrange("p n v k -> p n (v k)"),
                        in_=w_view[u, :, pair * CHUNKS : (pair + 1) * CHUNKS, :],
                    )

        def by_tensor(pair):
            return pair % 2 == 1 and pair < 2 * PAIRS_BY_TENSOR

        def regroup_by_tensor(pair):
            w_bank[pair] = w_bank_pool.tile([P, 2, P * WIN], BF16, name="w_bank")
            for n in range(2):
                nc.tensor.matmul(
                    out=w_bank[pair][:, n, :],
                    lhsT=identity_bf16[:],
                    rhs=w_raw[pair][:, CHUNKS - 2 + n, :, :].rearrange("p v k -> p k v"),
                    start=True,
                    stop=True,
                )

        def regroup_weights(job, on_scalar, on_vector):
            pair, k0, k1 = JOBS[job]
            if job in w_grouped:
                pass
            elif k1 - k0 == P:
                w_grouped[job] = w_grouped_pool.tile([P, CHUNKS, P, WIN], BF16, name="w_grouped", align_bytes=64)
            else:
                w_grouped[job] = w_half_pool.tile([P, CHUNKS, HALF, WIN], BF16, name="w_half", align_bytes=64)
            if k1 - k0 < P:
                k_scalar = K_SCALAR_HALVES[job - F0]
            else:
                k_scalar = K_SCALAR_FIRST if pair < FIRST_PAIRS else K_SCALAR if pair < FIRST_LATE_PAIR else K_SCALAR_LATE
            direct = CHUNKS
            if by_tensor(pair):
                direct = CHUNKS - 2
            if by_tensor(pair) and on_scalar:
                nc.scalar.copy(
                    out=w_grouped[job][:, direct:CHUNKS, :, :].rearrange("p n k v -> p n (k v)"),
                    in_=w_bank[pair][:],
                )
            if on_scalar:
              nc.scalar.copy(
                out=w_grouped[job][:, 0:direct, 0:k_scalar, :].rearrange("p n (q r) v -> p n q v r", r=4),
                in_=w_raw[pair][:, 0:direct, :, k0 : k0 + k_scalar].rearrange("p n v (q r) -> p n q v r", r=4),
            )
            if on_vector and k_scalar < k1 - k0:
              nc.vector.tensor_copy(
                out=w_grouped[job][:, 0:direct, k_scalar:, :].rearrange("p n (q r) v -> p n q v r", r=4),
                in_=w_raw[pair][:, 0:direct, :, k0 + k_scalar : k1].rearrange("p n v (q r) -> p n q v r", r=4),
            )

        def quantise_weights(job):
            width = CHUNKS * (JOBS[job][2] - JOBS[job][1])
            w_codes[job] = w_mx_pool.tile([P, width], U32, name="w_codes", align_bytes=64)
            w_scales[job] = w_mx_pool.tile([P, width], U8, name="w_scales", align_bytes=64)
            nc.vector.quantize_mx(
                out=w_codes[job][:].bitcast(FP8X4),
                scales=w_scales[job][:],
                in_=w_grouped[job][:].rearrange("p n k v -> p (n k v)"),
            )

        def first_window(g):
            some = slice(g * channels, (g + 1) * channels)
            for first in range(2):
                nc.vector.tensor_copy(
                    out=top[:, first, g * P : (g + 1) * P, :].rearrange("b (c r) w -> b c r w", r=WIN),
                    in_=image[:, some, 0:WIN, first : first + ROW_COLS],
                )
            for first in range(2):
                nc.vector.tensor_copy(
                    out=rows[:, :, first, g:P:PASSES, :],
                    in_=image[:, some, WIN:IMG, first : first + ROW_COLS].rearrange("b c r w -> b r c w"),
                )
            for s in range(PAIRS_IN_ROW):
                planes[g, s] = planes_pool.tile([P, PAIR, 2, P], F32, name="planes")
                for t in range(PAIR):
                    for h in range(2):
                        nc.tensor.transpose(planes[g, s][:, t, h, :], top_words[:, t, g * P : (g + 1) * P, s + h], identity[:])
            for s in range(PAIRS_IN_ROW):
                nc.scalar.copy(
                    out=ring_words[:, g, s, :, :, :],
                    in_=planes[g, s][:].rearrange("p t h b -> p t b h"),
                )

        def transpose_row(row, s):
            planes[row, s] = planes_pool.tile([P, PAIR, 2, P], F32, name="planes")
            for t in range(PAIR):
                for h in range(2):
                    nc.tensor.transpose(planes[row, s][:, t, h, :], rows_words[:, row - WIN, t, :, s + h], identity[:])

        def copy_out_row(row, s):
            if s == 0:
                x_rows[row] = x_pool.tile([P, OUT, P, WIN], BF16, name="x_row")
                x_words[row] = (
                    x_rows[row][:]
                    .rearrange("c j b v -> c (j b v)")
                    .bitcast(F32)
                    .rearrange("c (j b h) -> c j b h", j=OUT, h=2)
                )
            nc.scalar.copy(
                out=x_words[row][:, PAIR * s : PAIR * (s + 1), :, :],
                in_=planes[row, s][:].rearrange("c t h b -> c t b h"),
            )

        def spread_row(row):
            for g in range(PASSES):
                nc.sync.dma_start(
                    out=ring[row % WIN : P : WIN, g, :, :].rearrange("p j n -> p (j n)"),
                    in_=x_rows[row][g:P:PASSES].rearrange("c j b v -> c (j b v)"),
                )

        def quantise_patches(i, parts):
            if 0 in parts:
                patch_codes[i] = patch_mx_pool.tile([P, PASSES * OUT * P], U32, name="patch_codes", align_bytes=64)
                patch_scales[i] = patch_mx_pool.tile([P, PASSES * OUT * P], U8, name="patch_scales", align_bytes=64)
            width = CHUNKS * P
            for part in parts:
                cols = slice(part * width, (part + 1) * width)
                nc.vector.quantize_mx(
                    out=patch_codes[i][:, cols].bitcast(FP8X4),
                    scales=patch_scales[i][:, cols],
                    in_=ring[:].rearrange("p g j n -> p (g j n)")[:, cols.start * WIN : cols.stop * WIN],
                )

        def multiply(job):
            pair, k0, k1 = JOBS[job]
            bank = pair // 2 + (1 if k0 > 0 else 0)
            if pair % 2 == 0:
                acc[bank] = acc_pool.tile([P, 2 * PAIR, P], F32, name="acc")
            for t in range(PAIR):
                for g in range(PASSES):
                    first = (t * PASSES + g) * (k1 - k0)
                    if k1 - k0 == HALF and t == 1:
                        first -= HALF
                    cols = slice(first, first + P)
                    chunk = g * OUT + pair % PAIRS_IN_ROW * PAIR + t
                    patch_cols = slice(chunk * P, (chunk + 1) * P)
                    nc.tensor.matmul_mx(
                        out=acc[bank][:, (pair % 2) * PAIR + t, :],
                        lhsT=patch_codes[pair // PAIRS_IN_ROW][:, patch_cols].bitcast(FP8X4),
                        lhsT_scale=patch_scales[pair // PAIRS_IN_ROW][:, patch_cols],
                        rhs=w_codes[job][:, cols].bitcast(FP8X4),
                        rhs_scale=w_scales[job][:, cols],
                        start=(g == 0),
                        stop=(g == PASSES - 1),
                    )

        def copy_out_result(job):
            pair, k0, k1 = JOBS[job]
            bank = pair // 2 + (1 if k0 > 0 else 0)
            first = (pair - 1) * PAIR
            if k1 - k0 == P:
                nc.scalar.copy(
                    out=result[:, :, first : first + 2 * PAIR],
                    in_=acc[bank][:].rearrange("b q k -> b k q"),
                )
            else:
                nc.scalar.copy(
                    out=result[:, k0:k1, first : first + 2 * PAIR].rearrange("b k (r t) -> b k r t", t=PAIR),
                    in_=acc[bank][:]
                    .rearrange("b (r t) (h k) -> b r (t h) k", t=PAIR, h=2)[:, :, 0:4:3, :]
                    .rearrange("b r t k -> b k r t"),
                )
                nc.sync.dma_start(
                    out=out[:, k0:k1].rearrange("b k i j -> b (k i j)"),
                    in_=result[:, k0:k1, :].rearrange("b k q -> b (k q)"),
                )

        def exists(pair):
            return 0 <= pair < PAIRS

        def unit(step):
            return WIN + step // PAIRS_IN_ROW, step % PAIRS_IN_ROW

        units = (IMG - WIN) * PAIRS_IN_ROW

        make_identity(nc, identity[:])
        make_identity(nc, identity_bf16[:])
        load_image()
        for g in range(PASSES):
            first_window(g)
        quantise_patches(0, (0,))
        for step in range(-4, len(JOBS) + 1):
            load_weights(WIN * (step + 4 + 1))
            if 0 <= step - 1:
                multiply(step - 1)
            if 0 <= step + 4 < units:
                transpose_row(unit(step + 4)[0], unit(step + 4)[1])
            if 0 <= step + 3 < units:
                copy_out_row(unit(step + 3)[0], unit(step + 3)[1])
            if exists(step + 2) and by_tensor(step + 2):
                regroup_by_tensor(step + 2)
            if 0 <= step + 1 < FULL_PAIRS:
                regroup_weights(step + 1, True, True)
            for job in SCALAR_HALVES.get(step, []):
                regroup_weights(job, True, False)
            for job in VECTOR_HALVES.get(step, []):
                regroup_weights(job, False, True)
            if 0 <= step < len(JOBS):
                quantise_weights(step)
            if exists(step + 1) and (step + 1) % PAIRS_IN_ROW == 0:
                quantise_patches((step + 1) // PAIRS_IN_ROW, (1, 2) if step < 0 else (0, 1, 2))
            if 0 <= step + 3 < units and unit(step + 3)[1] == PAIRS_IN_ROW - 1:
                load_weights(WIN * (step + 4 + 1) + (1 if (step + 5) // PAIRS_IN_ROW % WIN > 0 else 0))
                spread_row(unit(step + 3)[0])
            if 0 <= step - 1 and JOBS[step - 1][0] % 2 == 1:
                copy_out_result(step - 1)
